import numpy as np
import ml_dtypes


def mxq(x, axis, fmt="e4m3"):
    dtype, down = {"e4m3": (ml_dtypes.float8_e4m3fn, 7), "e5m2": (ml_dtypes.float8_e5m2, 14)}[fmt]
    v = np.moveaxis(np.asarray(x, np.float32).astype(ml_dtypes.bfloat16).astype(np.float64), axis, -1)
    blocks = v.reshape(v.shape[:-1] + (-1, 32))
    amax = np.abs(blocks).max(-1, keepdims=True)
    byte = np.maximum(np.where(amax > 0, np.frexp(amax)[1] - 1 + 127, 0) - down, 1)
    scale = np.exp2(byte - 127.0)
    codes = (blocks / scale).astype(np.float32).astype(dtype).astype(np.float64)
    return np.moveaxis((codes * scale).reshape(v.shape), -1, axis)


WIDE = False


def mx_kscale(k):
    if not WIDE:
        return np.ones(k)
    levels = np.array([10, -10, 5, -5, 0])
    a = np.random.permutation(np.resize(levels, k // 512 * 4)).reshape(k // 512, 4)
    idx = np.arange(k)
    return np.exp2(a[idx // 512, idx % 128 // 32])


BF16 = ml_dtypes.bfloat16


def bf(x):
    return np.asarray(x, np.float32).astype(BF16)


def f64(x):
    return np.asarray(x).astype(np.float64)


E2M1 = np.array([0.0, 0.5, 1.0, 1.5, 2.0, 3.0, 4.0, 6.0, -0.0, -0.5, -1.0, -1.5, -2.0, -3.0, -4.0, -6.0])


def pack_weight(w, fmt):
    k, n = w.shape
    w = f64(bf(w)).reshape(k // 32, 32, n)
    amax = np.abs(w).max(1)
    if fmt == "e4m3":
        byte = np.frexp(amax)[1] - 1 + 127 - 7
    else:
        mant, ex = np.frexp(amax / 6.0)
        byte = np.where(mant > 0.5, ex, ex - 1) + 127
    byte = np.clip(np.where(amax > 0, byte, 1), 1, 254)
    scaled = (w * np.exp2(127.0 - byte)[:, None, :]).reshape(k, n).astype(np.float32)
    by_word = np.ascontiguousarray(scaled.reshape(k // 512, 128, 4, n).transpose(0, 1, 3, 2))
    if fmt == "e4m3":
        words = by_word.astype(ml_dtypes.float8_e4m3fn).view(np.uint8)
    else:
        c = by_word.astype(ml_dtypes.float4_e2m1fn).view(np.uint8) & 0xF
        words = c[..., 0::2] | (c[..., 1::2] << 4)
    return np.ascontiguousarray(words), np.ascontiguousarray(byte.astype(np.uint8).reshape(k // 512, 16, n))


def unpack_weight(words, scales, fmt):
    g, p, n, _ = words.shape
    if fmt == "e4m3":
        vals = np.ascontiguousarray(words).view(ml_dtypes.float8_e4m3fn).astype(np.float64)
    else:
        nib = np.empty((g, p, n, 4), np.uint8)
        nib[..., 0::2] = words & 0xF
        nib[..., 1::2] = words >> 4
        vals = E2M1[nib]
    vals = vals * np.repeat(np.exp2(scales.astype(np.float64) - 127.0), 8, axis=1)[..., None]
    return vals.transpose(0, 1, 3, 2).reshape(g * 512, n)


PAD_EPS = 1e-9
B, L, H, F = 2, 1024, 512, 2048
FMT = "e4m3"


def setup_inputs():
    s, t = mx_kscale(H), mx_kscale(F)
    x = bf(np.random.standard_normal((B, L, H)) * s)
    padding = bf(np.random.randint(0, 2, (B, L)))
    filter_weight_words, filter_weight_scales = pack_weight(np.random.standard_normal((H, F)) * 0.044 / s[:, None] * t, FMT)
    filter_bias = bf(np.random.standard_normal(F) * 0.1 * t)
    output_weight_words, output_weight_scales = pack_weight(np.random.standard_normal((F, H)) * 0.022 / t[:, None], FMT)
    output_bias = bf(np.random.standard_normal(H) * 0.1)
    return {"x": x,
            "padding": padding,
            "filter_weight_words": filter_weight_words,
            "filter_weight_scales": filter_weight_scales,
            "filter_bias": filter_bias,
            "output_weight_words": output_weight_words,
            "output_weight_scales": output_weight_scales,
            "output_bias": output_bias}


def reference(x, padding, filter_weight_words, filter_weight_scales, filter_bias, output_weight_words, output_weight_scales, output_bias):
    nonpad = (f64(padding) < PAD_EPS)[..., None]
    h = (mxq(f64(x), 2, "e4m3") @ unpack_weight(filter_weight_words, filter_weight_scales, FMT)) + f64(filter_bias)
    out = (mxq(h, 2, "e4m3") @ unpack_weight(output_weight_words, output_weight_scales, FMT)) + f64(output_bias)
    return np.where(nonpad, out, 0.0)

@@ -1,0 +1,284 @@
+from contextlib import ExitStack
+
+import concourse.mybir as mybir
+from concourse.masks import make_identity
+
+FLOPS = 2 * 2048 * 512 * 2048 * 2
+
+F32 = mybir.dt.float32
+BF16 = mybir.dt.bfloat16
+I32 = mybir.dt.int32
+U32 = mybir.dt.uint32
+U8 = mybir.dt.uint8
+FP8X4 = mybir.dt.float8_e4m3fn_x4
+ALU = mybir.AluOpType
+ACT = mybir.ActivationFunctionType
+
+P = 128
+NT = 16
+H = 512
+F = 2048
+NG = 4
+
+
+def tile_feedforwardnetwork_kernel(
+    tc,
+    x,
+    padding,
+    filter_weight_words,
+    filter_weight_scales,
+    filter_bias,
+    output_weight_words,
+    output_weight_scales,
+    output_bias,
+    out,
+):
+    nc = tc.nc
+    with ExitStack() as ctx:
+        ctx.enter_context(tc.manual_schedule())
+        keep = ctx.enter_context(tc.tile_pool(name="keep", bufs=1))
+        ring = ctx.enter_context(tc.tile_pool(name="ring", bufs=2))
+        psum = ctx.enter_context(tc.psum_pool(name="psum", bufs=1))
+
+        x_v = x.rearrange("b (q i) h -> (b q) i h", i=NT)
+        out_v = out.rearrange("b (q i) h -> (b q) i h", i=NT)
+        pad_v = padding.rearrange("b (q i) -> (b q) i", i=NT)
+
+        brow = keep.tile([P, F + H], BF16, name="brow")
+        ones = keep.tile([P, P], BF16, name="ones")
+        planes = keep.tile([P, 2 * F], U8, name="planes", align_bytes=64)
+        planes_i = planes[:].bitcast(I32)
+        nc.vector.memset(brow[:], 0.0)
+        nc.vector.memset(ones[:], 1.0)
+        nc.vector.memset(planes_i, 0)
+
+        pad_sb = keep.tile([P, NT], BF16, name="pad_sb")
+        nc.scalar.dma_start(out=brow[0:1, 0:F], in_=filter_bias.rearrange("(o f) -> o f", o=1))
+        nc.scalar.dma_start(out=brow[0:1, F : F + H], in_=output_bias.rearrange("(o f) -> o f", o=1))
+        nc.scalar.dma_start(out=pad_sb[:], in_=pad_v)
+
+        identf = keep.tile([P, P], F32, name="identf")
+        identb = keep.tile([P, P], BF16, name="identb")
+        make_identity(nc, identf[:])
+        make_identity(nc, identb[:])
+
+        x_sb = keep.tile([P, NT, H], BF16, name="x_sb")
+        w1 = keep.tile([P, F], U32, name="w1", align_bytes=64)
+        w2 = keep.tile([P, NG, H], U32, name="w2", align_bytes=64)
+        s1_i = filter_weight_scales.rearrange("o q n -> (o q) n").bitcast(I32)
+        s2_i = output_weight_scales.rearrange("g q n -> q g n").bitcast(I32)
+        w1_i = filter_weight_words.rearrange("o p n t -> (o p) (n t)").bitcast(I32)
+        w2_i = output_weight_words.rearrange("g p n t -> p g (n t)").bitcast(I32)
+
+        nc.sync.dma_start(out=x_sb[:, 0:2, :], in_=x_v[:, 0:2, :])
+        for r in range(4):
+            nc.sync.dma_start(out=planes_i[r:P:32, 0 : F // 4], in_=s1_i[r:16:4, :])
+        nc.sync.dma_start(out=w1[:, 0:1024].bitcast(I32), in_=w1_i[:, 0:1024])
+        nc.sync.dma_start(out=w1[:, 1024:2048].bitcast(I32), in_=w1_i[:, 1024:2048])
+        nc.sync.dma_start(out=x_sb[:, 2:8, :], in_=x_v[:, 2:8, :])
+        for r in range(4):
+            nc.sync.dma_start(
+                out=planes_i[r:P:32, F // 4 : F // 2].rearrange("p (g n) -> p g n", g=NG),
+                in_=s2_i[r:16:4, :, :],
+            )
+        nc.sync.dma_start(out=w2[:].bitcast(I32), in_=w2_i)
+        nc.sync.dma_start(out=x_sb[:, 8:16, :], in_=x_v[:, 8:16, :])
+
+        b1p = keep.tile([P, NG, 4, P], BF16, name="b1p")
+        b2bc = keep.tile([P, H], F32, name="b2bc")
+        b2m = keep.tile([P, NT, H], F32, name="b2m")
+        mask = keep.tile([P, NT], F32, name="mask")
+        xq = keep.tile([P, NT * P], U32, name="xq", align_bytes=64)
+        xs = keep.tile([P, NT * P], U8, name="xs", align_bytes=64)
+
+        def bias_mm(col, tag):
+            ps = psum.tile([P, 512], F32, name="bias_" + tag, tag=tag)
+            nc.tensor.matmul(out=ps[:], lhsT=ones[:], rhs=brow[:, col : col + 512], start=True, stop=True)
+            return ps
+
+        def by_t(ps):
+            return ps[:].rearrange("n (p t) -> n t p", t=4)
+
+        xts = {}
+        xgs = {}
+
+        def x_transpose(j, tag):
+            xt = psum.tile([P, 2, 2, P], F32, name="xt_" + tag, tag=tag)
+            for a in range(2):
+                words = x_sb[:, 2 * j + a, :].bitcast(F32)
+                for u in range(2):
+                    nc.tensor.transpose(xt[:, a, u, :], words[:, u : H // 2 : 2], identf[:])
+            xts[j] = xt
+
+        def x_evac(j, eng):
+            xg = ring.tile([P, 2, P, 4], BF16, name="xg", tag="xg", bufs=3, align_bytes=64)
+            src = xts[j][:].rearrange("p a u n -> p a n u")
+            if eng == "v":
+                nc.vector.tensor_copy(out=xg[:].bitcast(F32), in_=src)
+            else:
+                nc.scalar.copy(out=xg[:].bitcast(F32), in_=src)
+            xgs[j] = xg
+
+        def x_quant(j):
+            nc.vector.quantize_mx(
+                out=xq[:, 256 * j : 256 * (j + 1)].bitcast(FP8X4),
+                scales=xs[:, 256 * j : 256 * (j + 1)],
+                in_=xgs[j][:].rearrange("p a n t -> p (a n t)"),
+            )
+
+        hbs = {}
+        hsb = {}
+        tps = {}
+        grps = {}
+        hqs = {}
+        ybs = {}
+        ysb = {}
+
+        def layer1(i):
+            for g in range(NG):
+                hb = psum.tile([P, 512], F32, name="hb%d" % g, tag="hb%d" % g)
+                nc.tensor.matmul_mx(
+                    out=hb[:],
+                    lhsT=xq[:, P * i : P * (i + 1)].bitcast(FP8X4),
+                    lhsT_scale=xs[:, P * i : P * (i + 1)],
+                    rhs=w1[:, 512 * g : 512 * (g + 1)].bitcast(FP8X4),
+                    rhs_scale=planes[:, 512 * g : 512 * (g + 1)],
+                    start=True,
+                    stop=True,
+                )
+                hbs[(i, g)] = hb
+            hsb[i] = ring.tile([P, NG, 4, P], BF16, name="h_sb", tag="h_sb", bufs=3)
+
+        def evac1(i, g):
+            nc.vector.tensor_tensor(out=hsb[i][:, g], in0=by_t(hbs[(i, g)]), in1=b1p[:, g], op=ALU.add)
+
+        def h_transpose(i):
+            for half in range(2):
+                tp = psum.tile([P, 2, 4, P], BF16, name="tp%d" % half, tag="tp%d" % half)
+                for gg in range(2):
+                    for t in range(4):
+                        nc.tensor.transpose(tp[:, gg, t, :], hsb[i][:, 2 * half + gg, t, :], identb[:])
+                tps[(i, half)] = tp
+            grps[i] = ring.tile([P, NG, P, 4], BF16, name="grp", tag="grp", bufs=3, align_bytes=64)
+            hqs[i] = (
+                ring.tile([P, NG * P], U32, name="hq", tag="hq", bufs=3, align_bytes=64),
+                ring.tile([P, NG * P], U8, name="hs", tag="hs", bufs=3, align_bytes=64),
+            )
+
+        def evac2(i, half, eng):
+            src = tps[(i, half)][:].rearrange("p g t n -> p g n t")
+            dst = grps[i][:, 2 * half : 2 * half + 2]
+            if eng == "v":
+                nc.vector.tensor_copy(out=dst, in_=src)
+            else:
+                nc.scalar.copy(out=dst, in_=src)
+
+        def h_quant(i, half):
+            hq, hs = hqs[i]
+            nc.vector.quantize_mx(
+                out=hq[:, 256 * half : 256 * (half + 1)].bitcast(FP8X4),
+                scales=hs[:, 256 * half : 256 * (half + 1)],
+                in_=grps[i][:, 2 * half : 2 * half + 2].rearrange("p g n t -> p (g n t)"),
+            )
+
+        def layer2(i):
+            hq, hs = hqs[i]
+            yb = psum.tile([P, H], F32, name="yb", tag="yb")
+            for g in range(NG):
+                nc.tensor.matmul_mx(
+                    out=yb[:],
+                    lhsT=hq[:, P * g : P * (g + 1)].bitcast(FP8X4),
+                    lhsT_scale=hs[:, P * g : P * (g + 1)],
+                    rhs=w2[:, g, :].bitcast(FP8X4),
+                    rhs_scale=planes[:, F + H * g : F + H * (g + 1)],
+                    start=(g == 0),
+                    stop=(g == NG - 1),
+                )
+            ybs[i] = yb
+
+        def masked_bias(i):
+            nc.gpsimd.tensor_scalar(
+                out=b2m[:, i, :],
+                in0=b2bc[:],
+                scalar1=mask[:, i : i + 1],
+                scalar2=0.0,
+                op0=ALU.mult,
+                op1=ALU.add,
+            )
+
+        def evac3(i, on_vector):
+            y = ring.tile([P, H], F32, name="y_sb", tag="y_sb", bufs=3)
+            if on_vector:
+                nc.vector.scalar_tensor_tensor(
+                    out=y[:],
+                    in0=ybs[i][:],
+                    scalar=mask[:, i : i + 1],
+                    in1=b2m[:, i, :],
+                    op0=ALU.mult,
+                    op1=ALU.add,
+                )
+            else:
+                nc.scalar.activation(out=y[:], in_=ybs[i][:], func=ACT.Copy, scale=mask[:, i : i + 1])
+                nc.gpsimd.tensor_tensor(out=y[:], in0=y[:], in1=b2m[:, i, :], op=ALU.add)
+            nc.sync.dma_start(out=out_v[:, i, :], in_=y[:])
+
+        ps0 = bias_mm(0, "yb")
+        ps1 = bias_mm(512, "xb")
+        nc.vector.tensor_copy(out=b1p[:, 0], in_=by_t(ps0))
+        nc.scalar.copy(out=b1p[:, 1], in_=by_t(ps1))
+        nc.vector.tensor_single_scalar(out=mask[:], in_=pad_sb[:], scalar=1e-9, op=ALU.is_lt)
+        x_transpose(0, "hb0")
+        x_transpose(1, "hb1")
+        x_evac(0, "v")
+        x_evac(1, "s")
+        x_quant(0)
+        ps2 = bias_mm(1024, "tp0")
+        ps3 = bias_mm(1536, "tp1")
+        ps4 = bias_mm(2048, "hb2")
+        nc.scalar.copy(out=b1p[:, 2], in_=by_t(ps2))
+        nc.scalar.copy(out=b1p[:, 3], in_=by_t(ps3))
+        nc.scalar.activation(out=b2bc[:], in_=ps4[:], func=ACT.Copy)
+        masked_bias(0)
+        masked_bias(1)
+
+        layer1(0)
+        evac1(0, 0)
+        evac1(0, 1)
+        x_quant(1)
+        evac1(0, 2)
+        evac1(0, 3)
+        x_transpose(2, "xb")
+        x_transpose(3, "yb")
+        x_evac(2, "s")
+        x_evac(3, "s")
+
+        for s in range(NT + 1):
+            if s >= 1:
+                h_quant(s - 1, 0)
+            if s + 1 < NT:
+                layer1(s + 1)
+                evac1(s + 1, 0)
+            if s >= 1:
+                h_quant(s - 1, 1)
+            if s + 1 < NT:
+                evac1(s + 1, 1)
+                if s == 0:
+                    x_quant(2)
+                    x_quant(3)
+                if 1 <= s <= 4:
+                    x_quant(s + 3)
+                evac1(s + 1, 2)
+                evac1(s + 1, 3)
+            if s < NT:
+                h_transpose(s)
+                last = s == NT - 1
+                evac2(s, 0, "s")
+                evac2(s, 1, "v" if last else "s")
+            if s <= 3:
+                x_transpose(s + 4, "xb")
+                x_evac(s + 4, "s")
+            if s >= 1:
+                layer2(s - 1)
+                evac3(s - 1, s - 1 == NT - 1)
+            if s + 2 < NT:
+                masked_bias(s + 2)

@@ -56,6 +56,8 @@ def tile_feedforwardnetwork_kernel(
         nc.scalar.dma_start(out=brow[0:1, 0:F], in_=filter_bias.rearrange("(o f) -> o f", o=1))
         nc.scalar.dma_start(out=brow[0:1, F : F + H], in_=output_bias.rearrange("(o f) -> o f", o=1))
         nc.scalar.dma_start(out=pad_sb[:], in_=pad_v)
+        warm = keep.tile([P, 1], F32, name="warm")
+        nc.scalar.activation(out=warm[:], in_=ones[:, 0:1], func=ACT.Copy)
 
         identf = keep.tile([P, P], F32, name="identf")
         identb = keep.tile([P, P], BF16, name="identb")
@@ -76,13 +78,13 @@ def tile_feedforwardnetwork_kernel(
         nc.sync.dma_start(out=w1[:, 0:1024].bitcast(I32), in_=w1_i[:, 0:1024])
         nc.sync.dma_start(out=w1[:, 1024:2048].bitcast(I32), in_=w1_i[:, 1024:2048])
         nc.sync.dma_start(out=x_sb[:, 2:8, :], in_=x_v[:, 2:8, :])
+        nc.sync.dma_start(out=x_sb[:, 8:16, :], in_=x_v[:, 8:16, :])
         for r in range(4):
             nc.sync.dma_start(
                 out=planes_i[r:P:32, F // 4 : F // 2].rearrange("p (g n) -> p g n", g=NG),
                 in_=s2_i[r:16:4, :, :],
             )
         nc.sync.dma_start(out=w2[:].bitcast(I32), in_=w2_i)
-        nc.sync.dma_start(out=x_sb[:, 8:16, :], in_=x_v[:, 8:16, :])
 
         b1p = keep.tile([P, NG, 4, P], BF16, name="b1p")
         b2bc = keep.tile([P, H], F32, name="b2bc")
@@ -111,7 +113,7 @@ def tile_feedforwardnetwork_kernel(
             xts[j] = xt
 
         def x_evac(j, eng):
-            xg = ring.tile([P, 2, P, 4], BF16, name="xg", tag="xg", bufs=3, align_bytes=64)
+            xg = ring.tile([P, 2, P, 4], BF16, name="xg", tag="xg", bufs=8, align_bytes=64)
             src = xts[j][:].rearrange("p a u n -> p a n u")
             if eng == "v":
                 nc.vector.tensor_copy(out=xg[:].bitcast(F32), in_=src)
@@ -234,12 +236,12 @@ def tile_feedforwardnetwork_kernel(
         x_quant(0)
         ps2 = bias_mm(1024, "tp0")
         ps3 = bias_mm(1536, "tp1")
-        ps4 = bias_mm(2048, "hb2")
+        ps4 = bias_mm(2048, "yb")
         nc.scalar.copy(out=b1p[:, 2], in_=by_t(ps2))
         nc.scalar.copy(out=b1p[:, 3], in_=by_t(ps3))
         nc.scalar.activation(out=b2bc[:], in_=ps4[:], func=ACT.Copy)
-        masked_bias(0)
-        masked_bias(1)
+        for i in range(NT):
+            masked_bias(i)
 
         layer1(0)
         evac1(0, 0)
@@ -247,8 +249,8 @@ def tile_feedforwardnetwork_kernel(
         x_quant(1)
         evac1(0, 2)
         evac1(0, 3)
-        x_transpose(2, "xb")
-        x_transpose(3, "yb")
+        x_transpose(2, "tp0")
+        x_transpose(3, "tp1")
         x_evac(2, "s")
         x_evac(3, "s")
 
@@ -262,11 +264,11 @@ def tile_feedforwardnetwork_kernel(
                 h_quant(s - 1, 1)
             if s + 1 < NT:
                 evac1(s + 1, 1)
-                if s == 0:
-                    x_quant(2)
-                    x_quant(3)
-                if 1 <= s <= 4:
-                    x_quant(s + 3)
+                if s <= 1:
+                    x_quant(2 * s + 2)
+                    x_quant(2 * s + 3)
+                if 2 <= s <= 3:
+                    x_quant(s + 4)
                 evac1(s + 1, 2)
                 evac1(s + 1, 3)
             if s < NT:
@@ -274,11 +276,14 @@ def tile_feedforwardnetwork_kernel(
                 last = s == NT - 1
                 evac2(s, 0, "s")
                 evac2(s, 1, "v" if last else "s")
-            if s <= 3:
-                x_transpose(s + 4, "xb")
-                x_evac(s + 4, "s")
+            if s == 0:
+                x_transpose(4, "xb")
+                x_transpose(5, "yb")
+                x_evac(4, "s")
+                x_evac(5, "s")
+            if 1 <= s <= 2:
+                x_transpose(s + 5, "xb")
+                x_evac(s + 5, "s")
             if s >= 1:
                 layer2(s - 1)
                 evac3(s - 1, s - 1 == NT - 1)
-            if s + 2 < NT:
-                masked_bias(s + 2)

@@ -16,9 +16,14 @@ ACT = mybir.ActivationFunctionType
 
 P = 128
 NT = 16
+NB = 4
+TB = 512
 H = 512
 F = 2048
 NG = 4
+
+V_SHARE = (8, 5, 0, 0)
+E3_ON_VECTOR_FROM = 12
 
 
 def tile_feedforwardnetwork_kernel(
@@ -35,29 +40,33 @@ def tile_feedforwardnetwork_kernel(
 ):
     nc = tc.nc
     with ExitStack() as ctx:
-        ctx.enter_context(tc.manual_schedule())
         keep = ctx.enter_context(tc.tile_pool(name="keep", bufs=1))
         ring = ctx.enter_context(tc.tile_pool(name="ring", bufs=2))
-        psum = ctx.enter_context(tc.psum_pool(name="psum", bufs=1))
+        ps_h = ctx.enter_context(tc.psum_pool(name="ps_h", bufs=4))
+        ps_y = ctx.enter_context(tc.psum_pool(name="ps_y", bufs=4))
 
         x_v = x.rearrange("b (q i) h -> (b q) i h", i=NT)
         out_v = out.rearrange("b (q i) h -> (b q) i h", i=NT)
         pad_v = padding.rearrange("b (q i) -> (b q) i", i=NT)
 
-        brow = keep.tile([P, F + H], BF16, name="brow")
+        brows = keep.tile([P, P], BF16, name="brows")
+        brow2 = keep.tile([P, H], BF16, name="brow2")
         ones = keep.tile([P, P], BF16, name="ones")
         planes = keep.tile([P, 2 * F], U8, name="planes", align_bytes=64)
         planes_i = planes[:].bitcast(I32)
-        nc.vector.memset(brow[:], 0.0)
+        nc.vector.memset(brows[:], 0.0)
+        nc.vector.memset(brow2[:], 0.0)
         nc.vector.memset(ones[:], 1.0)
         nc.vector.memset(planes_i, 0)
 
         pad_sb = keep.tile([P, NT], BF16, name="pad_sb")
-        nc.scalar.dma_start(out=brow[0:1, 0:F], in_=filter_bias.rearrange("(o f) -> o f", o=1))
-        nc.scalar.dma_start(out=brow[0:1, F : F + H], in_=output_bias.rearrange("(o f) -> o f", o=1))
+        for g in range(NG):
+            nc.scalar.dma_start(
+                out=brows[4 * g : 4 * g + 4, :].rearrange("c (a r) -> c a r", r=4),
+                in_=filter_bias[512 * g : 512 * (g + 1)].rearrange("(a c r) -> c a r", c=4, r=4),
+            )
+        nc.scalar.dma_start(out=brow2[0:1, :], in_=output_bias.rearrange("(o f) -> o f", o=1))
         nc.scalar.dma_start(out=pad_sb[:], in_=pad_v)
-        warm = keep.tile([P, 1], F32, name="warm")
-        nc.scalar.activation(out=warm[:], in_=ones[:, 0:1], func=ACT.Copy)
 
         identf = keep.tile([P, P], F32, name="identf")
         identb = keep.tile([P, P], BF16, name="identb")
@@ -65,138 +74,101 @@ def tile_feedforwardnetwork_kernel(
         make_identity(nc, identb[:])
 
         x_sb = keep.tile([P, NT, H], BF16, name="x_sb")
+        w1raw = keep.tile([P, F], U32, name="w1raw")
         w1 = keep.tile([P, F], U32, name="w1", align_bytes=64)
+        s1 = keep.tile([P, F], U8, name="s1", align_bytes=64)
         w2 = keep.tile([P, NG, H], U32, name="w2", align_bytes=64)
         s1_i = filter_weight_scales.rearrange("o q n -> (o q) n").bitcast(I32)
         s2_i = output_weight_scales.rearrange("g q n -> q g n").bitcast(I32)
         w1_i = filter_weight_words.rearrange("o p n t -> (o p) (n t)").bitcast(I32)
         w2_i = output_weight_words.rearrange("g p n t -> p g (n t)").bitcast(I32)
 
-        nc.sync.dma_start(out=x_sb[:, 0:2, :], in_=x_v[:, 0:2, :])
+        nc.sync.dma_start(out=x_sb[:, 0:4, :], in_=x_v[:, 0:4, :])
         for r in range(4):
             nc.sync.dma_start(out=planes_i[r:P:32, 0 : F // 4], in_=s1_i[r:16:4, :])
-        nc.sync.dma_start(out=w1[:, 0:1024].bitcast(I32), in_=w1_i[:, 0:1024])
-        nc.sync.dma_start(out=w1[:, 1024:2048].bitcast(I32), in_=w1_i[:, 1024:2048])
-        nc.sync.dma_start(out=x_sb[:, 2:8, :], in_=x_v[:, 2:8, :])
-        nc.sync.dma_start(out=x_sb[:, 8:16, :], in_=x_v[:, 8:16, :])
+        nc.sync.dma_start(out=w1raw[:, 0:1024].bitcast(I32), in_=w1_i[:, 0:1024])
+        nc.sync.dma_start(out=w1raw[:, 1024:2048].bitcast(I32), in_=w1_i[:, 1024:2048])
+        nc.sync.dma_start(out=x_sb[:, 4:8, :], in_=x_v[:, 4:8, :])
         for r in range(4):
             nc.sync.dma_start(
                 out=planes_i[r:P:32, F // 4 : F // 2].rearrange("p (g n) -> p g n", g=NG),
                 in_=s2_i[r:16:4, :, :],
             )
         nc.sync.dma_start(out=w2[:].bitcast(I32), in_=w2_i)
+        nc.sync.dma_start(out=x_sb[:, 8:16, :], in_=x_v[:, 8:16, :])
 
-        b1p = keep.tile([P, NG, 4, P], BF16, name="b1p")
+        b1col = keep.tile([P, 16], F32, name="b1col")
         b2bc = keep.tile([P, H], F32, name="b2bc")
-        b2m = keep.tile([P, NT, H], F32, name="b2m")
+        b2m = keep.tile([P, NT, H], BF16, name="b2m")
         mask = keep.tile([P, NT], F32, name="mask")
         xq = keep.tile([P, NT * P], U32, name="xq", align_bytes=64)
         xs = keep.tile([P, NT * P], U8, name="xs", align_bytes=64)
 
-        def bias_mm(col, tag):
-            ps = psum.tile([P, 512], F32, name="bias_" + tag, tag=tag)
-            nc.tensor.matmul(out=ps[:], lhsT=ones[:], rhs=brow[:, col : col + 512], start=True, stop=True)
-            return ps
+        nc.vector.tensor_single_scalar(out=mask[:], in_=pad_sb[:], scalar=1e-9, op=ALU.is_lt)
+        bt = ps_h.tile([P, P], BF16, name="bt", tag="hb")
+        nc.tensor.transpose(bt[:], brows[:], identb[:])
+        nc.vector.tensor_copy(out=b1col[:], in_=bt[:, 0:16])
+        b2ps = ps_y.tile([P, H], F32, name="b2ps", tag="yb")
+        nc.tensor.matmul(out=b2ps[:], lhsT=ones[:], rhs=brow2[:], start=True, stop=True)
+        nc.scalar.activation(out=b2bc[:], in_=b2ps[:], func=ACT.Copy)
 
-        def by_t(ps):
-            return ps[:].rearrange("n (p t) -> n t p", t=4)
+        nc.vector.tensor_copy(
+            out=s1[:].bitcast(I32).rearrange("p (g c a) -> p g c a", g=NG, c=4),
+            in_=planes_i[:, 0 : F // 4].rearrange("p (g a c) -> p g c a", g=NG, c=4),
+        )
 
-        xts = {}
-        xgs = {}
+        def permute_w1(g):
+            cols = slice(512 * g, 512 * (g + 1))
+            nc.vector.tensor_copy(
+                out=w1[:, cols].bitcast(I32).rearrange("p (c a r) -> p c a r", c=4, r=4),
+                in_=w1raw[:, cols].bitcast(I32).rearrange("p (a c r) -> p c a r", c=4, r=4),
+            )
 
-        def x_transpose(j, tag):
-            xt = psum.tile([P, 2, 2, P], F32, name="xt_" + tag, tag=tag)
+        def x_pair(j, eng):
+            xt = ps_h.tile([P, 2, 2, P], F32, name="xt", tag="hb")
             for a in range(2):
                 words = x_sb[:, 2 * j + a, :].bitcast(F32)
                 for u in range(2):
                     nc.tensor.transpose(xt[:, a, u, :], words[:, u : H // 2 : 2], identf[:])
-            xts[j] = xt
-
-        def x_evac(j, eng):
-            xg = ring.tile([P, 2, P, 4], BF16, name="xg", tag="xg", bufs=8, align_bytes=64)
-            src = xts[j][:].rearrange("p a u n -> p a n u")
+            xg = ring.tile([P, 2, P, 4], BF16, name="xg", tag="xg", bufs=4, align_bytes=64)
+            src = xt[:].rearrange("p a u n -> p a n u")
             if eng == "v":
                 nc.vector.tensor_copy(out=xg[:].bitcast(F32), in_=src)
             else:
                 nc.scalar.copy(out=xg[:].bitcast(F32), in_=src)
-            xgs[j] = xg
-
-        def x_quant(j):
             nc.vector.quantize_mx(
                 out=xq[:, 256 * j : 256 * (j + 1)].bitcast(FP8X4),
                 scales=xs[:, 256 * j : 256 * (j + 1)],
-                in_=xgs[j][:].rearrange("p a n t -> p (a n t)"),
+                in_=xg[:].rearrange("p a n t -> p (a n t)"),
             )
 
-        hbs = {}
-        hsb = {}
-        tps = {}
-        grps = {}
-        hqs = {}
-        ybs = {}
-        ysb = {}
+        folded = {}
 
-        def layer1(i):
-            for g in range(NG):
-                hb = psum.tile([P, 512], F32, name="hb%d" % g, tag="hb%d" % g)
-                nc.tensor.matmul_mx(
-                    out=hb[:],
-                    lhsT=xq[:, P * i : P * (i + 1)].bitcast(FP8X4),
-                    lhsT_scale=xs[:, P * i : P * (i + 1)],
-                    rhs=w1[:, 512 * g : 512 * (g + 1)].bitcast(FP8X4),
-                    rhs_scale=planes[:, 512 * g : 512 * (g + 1)],
-                    start=True,
-                    stop=True,
-                )
-                hbs[(i, g)] = hb
-            hsb[i] = ring.tile([P, NG, 4, P], BF16, name="h_sb", tag="h_sb", bufs=3)
-
-        def evac1(i, g):
-            nc.vector.tensor_tensor(out=hsb[i][:, g], in0=by_t(hbs[(i, g)]), in1=b1p[:, g], op=ALU.add)
-
-        def h_transpose(i):
-            for half in range(2):
-                tp = psum.tile([P, 2, 4, P], BF16, name="tp%d" % half, tag="tp%d" % half)
-                for gg in range(2):
-                    for t in range(4):
-                        nc.tensor.transpose(tp[:, gg, t, :], hsb[i][:, 2 * half + gg, t, :], identb[:])
-                tps[(i, half)] = tp
-            grps[i] = ring.tile([P, NG, P, 4], BF16, name="grp", tag="grp", bufs=3, align_bytes=64)
-            hqs[i] = (
-                ring.tile([P, NG * P], U32, name="hq", tag="hq", bufs=3, align_bytes=64),
-                ring.tile([P, NG * P], U8, name="hs", tag="hs", bufs=3, align_bytes=64),
-            )
-
-        def evac2(i, half, eng):
-            src = tps[(i, half)][:].rearrange("p g t n -> p g n t")
-            dst = grps[i][:, 2 * half : 2 * half + 2]
-            if eng == "v":
-                nc.vector.tensor_copy(out=dst, in_=src)
-            else:
-                nc.scalar.copy(out=dst, in_=src)
-
-        def h_quant(i, half):
-            hq, hs = hqs[i]
-            nc.vector.quantize_mx(
-                out=hq[:, 256 * half : 256 * (half + 1)].bitcast(FP8X4),
-                scales=hs[:, 256 * half : 256 * (half + 1)],
-                in_=grps[i][:, 2 * half : 2 * half + 2].rearrange("p g n t -> p (g n t)"),
-            )
-
-        def layer2(i):
-            hq, hs = hqs[i]
-            yb = psum.tile([P, H], F32, name="yb", tag="yb")
-            for g in range(NG):
-                nc.tensor.matmul_mx(
-                    out=yb[:],
-                    lhsT=hq[:, P * g : P * (g + 1)].bitcast(FP8X4),
-                    lhsT_scale=hs[:, P * g : P * (g + 1)],
-                    rhs=w2[:, g, :].bitcast(FP8X4),
-                    rhs_scale=planes[:, F + H * g : F + H * (g + 1)],
-                    start=(g == 0),
-                    stop=(g == NG - 1),
-                )
-            ybs[i] = yb
+        def layer1(b):
+            ht = ring.tile([P, 16, TB], BF16, name="ht", tag="ht", bufs=3)
+            rt = ring.tile([P, NG, 4, TB], BF16, name="rt", tag="rt", bufs=2)
+            k = 0
+            for cq in range(4):
+                for g in range(NG):
+                    c = 4 * g + cq
+                    hb = ps_h.tile([P, TB], F32, name="hb", tag="hb")
+                    nc.tensor.matmul_mx(
+                        out=hb[:],
+                        lhsT=w1[:, P * c : P * (c + 1)].bitcast(FP8X4),
+                        lhsT_scale=s1[:, P * c : P * (c + 1)],
+                        rhs=xq[:, TB * b : TB * (b + 1)].bitcast(FP8X4),
+                        rhs_scale=xs[:, TB * b : TB * (b + 1)],
+                        start=True,
+                        stop=True,
+                    )
+                    if k % 2 == 1 and k // 2 < V_SHARE[b]:
+                        nc.vector.tensor_scalar_add(out=ht[:, c, :], in0=hb[:], scalar1=b1col[:, c : c + 1])
+                    else:
+                        nc.scalar.activation(out=ht[:, c, :], in_=hb[:], func=ACT.Identity, bias=b1col[:, c : c + 1])
+                    k += 1
+                for t in range(4):
+                    nc.sync.dma_start(out=rt[cq:P:4, :, t, :], in_=ht[t:P:4, cq:16:4, :])
+            folded[b] = rt
 
         def masked_bias(i):
             nc.gpsimd.tensor_scalar(
@@ -208,82 +180,65 @@ def tile_feedforwardnetwork_kernel(
                 op1=ALU.add,
             )
 
-        def evac3(i, on_vector):
-            y = ring.tile([P, H], F32, name="y_sb", tag="y_sb", bufs=3)
-            if on_vector:
-                nc.vector.scalar_tensor_tensor(
-                    out=y[:],
-                    in0=ybs[i][:],
-                    scalar=mask[:, i : i + 1],
-                    in1=b2m[:, i, :],
-                    op0=ALU.mult,
-                    op1=ALU.add,
-                )
-            else:
-                nc.scalar.activation(out=y[:], in_=ybs[i][:], func=ACT.Copy, scale=mask[:, i : i + 1])
-                nc.gpsimd.tensor_tensor(out=y[:], in0=y[:], in1=b2m[:, i, :], op=ALU.add)
-            nc.sync.dma_start(out=out_v[:, i, :], in_=y[:])
+        def regroup(b, g):
+            grp = ring.tile([P, TB, 4], BF16, name="grp", tag="grp", bufs=3, align_bytes=64)
+            nc.vector.tensor_copy(out=grp[:], in_=folded[b][:, g].rearrange("p t n -> p n t"))
+            return grp
 
-        ps0 = bias_mm(0, "yb")
-        ps1 = bias_mm(512, "xb")
-        nc.vector.tensor_copy(out=b1p[:, 0], in_=by_t(ps0))
-        nc.scalar.copy(out=b1p[:, 1], in_=by_t(ps1))
-        nc.vector.tensor_single_scalar(out=mask[:], in_=pad_sb[:], scalar=1e-9, op=ALU.is_lt)
-        x_transpose(0, "hb0")
-        x_transpose(1, "hb1")
-        x_evac(0, "v")
-        x_evac(1, "s")
-        x_quant(0)
-        ps2 = bias_mm(1024, "tp0")
-        ps3 = bias_mm(1536, "tp1")
-        ps4 = bias_mm(2048, "yb")
-        nc.scalar.copy(out=b1p[:, 2], in_=by_t(ps2))
-        nc.scalar.copy(out=b1p[:, 3], in_=by_t(ps3))
-        nc.scalar.activation(out=b2bc[:], in_=ps4[:], func=ACT.Copy)
+        def layer2(b):
+            hq = ring.tile([P, NG, TB], U32, name="hq", tag="hq", bufs=2, align_bytes=64)
+            hs = ring.tile([P, NG, TB], U8, name="hs", tag="hs", bufs=2, align_bytes=64)
+            ybs = []
+            for ii in range(4):
+                ybs.append(ps_y.tile([P, H], F32, name="yb", tag="yb"))
+            grps = [regroup(b, 0)]
+            for g in range(NG):
+                if g + 1 < NG:
+                    grps.append(regroup(b, g + 1))
+                nc.vector.quantize_mx(
+                    out=hq[:, g, :].bitcast(FP8X4),
+                    scales=hs[:, g, :],
+                    in_=grps[g][:].rearrange("p n t -> p (n t)"),
+                )
+                for ii in range(4):
+                    nc.tensor.matmul_mx(
+                        out=ybs[ii][:],
+                        lhsT=hq[:, g, P * ii : P * (ii + 1)].bitcast(FP8X4),
+                        lhsT_scale=hs[:, g, P * ii : P * (ii + 1)],
+                        rhs=w2[:, g, :].bitcast(FP8X4),
+                        rhs_scale=planes[:, F + H * g : F + H * (g + 1)],
+                        start=(g == 0),
+                        stop=(g == NG - 1),
+                    )
+            for ii in range(4):
+                i = 4 * b + ii
+                y = ring.tile([P, H], F32, name="y_sb", tag="y_sb", bufs=4)
+                if i >= E3_ON_VECTOR_FROM:
+                    nc.vector.scalar_tensor_tensor(
+                        out=y[:],
+                        in0=ybs[ii][:],
+                        scalar=mask[:, i : i + 1],
+                        in1=b2m[:, i, :],
+                        op0=ALU.mult,
+                        op1=ALU.add,
+                    )
+                else:
+                    nc.scalar.activation(out=y[:], in_=ybs[ii][:], func=ACT.Copy, scale=mask[:, i : i + 1])
+                    nc.gpsimd.tensor_tensor(out=y[:], in0=y[:], in1=b2m[:, i, :], op=ALU.add)
+                nc.sync.dma_start(out=out_v[:, i, :], in_=y[:])
+
+        permute_w1(0)
+        x_pair(0, "v")
+        x_pair(1, "s")
+        for g in range(1, NG):
+            permute_w1(g)
         for i in range(NT):
             masked_bias(i)
-
-        layer1(0)
-        evac1(0, 0)
-        evac1(0, 1)
-        x_quant(1)
-        evac1(0, 2)
-        evac1(0, 3)
-        x_transpose(2, "tp0")
-        x_transpose(3, "tp1")
-        x_evac(2, "s")
-        x_evac(3, "s")
-
-        for s in range(NT + 1):
-            if s >= 1:
-                h_quant(s - 1, 0)
-            if s + 1 < NT:
-                layer1(s + 1)
-                evac1(s + 1, 0)
-            if s >= 1:
-                h_quant(s - 1, 1)
-            if s + 1 < NT:
-                evac1(s + 1, 1)
-                if s <= 1:
-                    x_quant(2 * s + 2)
-                    x_quant(2 * s + 3)
-                if 2 <= s <= 3:
-                    x_quant(s + 4)
-                evac1(s + 1, 2)
-                evac1(s + 1, 3)
-            if s < NT:
-                h_transpose(s)
-                last = s == NT - 1
-                evac2(s, 0, "s")
-                evac2(s, 1, "v" if last else "s")
-            if s == 0:
-                x_transpose(4, "xb")
-                x_transpose(5, "yb")
-                x_evac(4, "s")
-                x_evac(5, "s")
-            if 1 <= s <= 2:
-                x_transpose(s + 5, "xb")
-                x_evac(s + 5, "s")
-            if s >= 1:
-                layer2(s - 1)
-                evac3(s - 1, s - 1 == NT - 1)
+        for b in range(NB):
+            layer1(b)
+            if b + 1 < NB:
+                x_pair(2 * b + 2, "s")
+                x_pair(2 * b + 3, "s")
+            if b >= 1:
+                layer2(b - 1)
+        layer2(NB - 1)

@@ -16,14 +16,10 @@ ACT = mybir.ActivationFunctionType
 
 P = 128
 NT = 16
-NB = 4
-TB = 512
 H = 512
 F = 2048
 NG = 4
-
-V_SHARE = (8, 5, 0, 0)
-E3_ON_VECTOR_FROM = 12
+TP_BANKS = ("tp0", "tp1", "xb")
 
 
 def tile_feedforwardnetwork_kernel(
@@ -40,33 +36,29 @@ def tile_feedforwardnetwork_kernel(
 ):
     nc = tc.nc
     with ExitStack() as ctx:
+        ctx.enter_context(tc.manual_schedule())
         keep = ctx.enter_context(tc.tile_pool(name="keep", bufs=1))
         ring = ctx.enter_context(tc.tile_pool(name="ring", bufs=2))
-        ps_h = ctx.enter_context(tc.psum_pool(name="ps_h", bufs=4))
-        ps_y = ctx.enter_context(tc.psum_pool(name="ps_y", bufs=4))
+        psum = ctx.enter_context(tc.psum_pool(name="psum", bufs=1))
 
         x_v = x.rearrange("b (q i) h -> (b q) i h", i=NT)
         out_v = out.rearrange("b (q i) h -> (b q) i h", i=NT)
         pad_v = padding.rearrange("b (q i) -> (b q) i", i=NT)
 
-        brows = keep.tile([P, P], BF16, name="brows")
-        brow2 = keep.tile([P, H], BF16, name="brow2")
+        brow = keep.tile([P, F + H], BF16, name="brow")
         ones = keep.tile([P, P], BF16, name="ones")
         planes = keep.tile([P, 2 * F], U8, name="planes", align_bytes=64)
         planes_i = planes[:].bitcast(I32)
-        nc.vector.memset(brows[:], 0.0)
-        nc.vector.memset(brow2[:], 0.0)
+        nc.vector.memset(brow[:], 0.0)
         nc.vector.memset(ones[:], 1.0)
         nc.vector.memset(planes_i, 0)
 
         pad_sb = keep.tile([P, NT], BF16, name="pad_sb")
-        for g in range(NG):
-            nc.scalar.dma_start(
-                out=brows[4 * g : 4 * g + 4, :].rearrange("c (a r) -> c a r", r=4),
-                in_=filter_bias[512 * g : 512 * (g + 1)].rearrange("(a c r) -> c a r", c=4, r=4),
-            )
-        nc.scalar.dma_start(out=brow2[0:1, :], in_=output_bias.rearrange("(o f) -> o f", o=1))
+        nc.scalar.dma_start(out=brow[0:1, 0:F], in_=filter_bias.rearrange("(o f) -> o f", o=1))
+        nc.scalar.dma_start(out=brow[0:1, F : F + H], in_=output_bias.rearrange("(o f) -> o f", o=1))
         nc.scalar.dma_start(out=pad_sb[:], in_=pad_v)
+        warm = keep.tile([P, 1], F32, name="warm")
+        nc.scalar.activation(out=warm[:], in_=ones[:, 0:1], func=ACT.Copy)
 
         identf = keep.tile([P, P], F32, name="identf")
         identb = keep.tile([P, P], BF16, name="identb")
@@ -74,101 +66,139 @@ def tile_feedforwardnetwork_kernel(
         make_identity(nc, identb[:])
 
         x_sb = keep.tile([P, NT, H], BF16, name="x_sb")
-        w1raw = keep.tile([P, F], U32, name="w1raw")
         w1 = keep.tile([P, F], U32, name="w1", align_bytes=64)
-        s1 = keep.tile([P, F], U8, name="s1", align_bytes=64)
         w2 = keep.tile([P, NG, H], U32, name="w2", align_bytes=64)
         s1_i = filter_weight_scales.rearrange("o q n -> (o q) n").bitcast(I32)
         s2_i = output_weight_scales.rearrange("g q n -> q g n").bitcast(I32)
         w1_i = filter_weight_words.rearrange("o p n t -> (o p) (n t)").bitcast(I32)
         w2_i = output_weight_words.rearrange("g p n t -> p g (n t)").bitcast(I32)
 
-        nc.sync.dma_start(out=x_sb[:, 0:4, :], in_=x_v[:, 0:4, :])
+        nc.sync.dma_start(out=x_sb[:, 0:2, :], in_=x_v[:, 0:2, :])
         for r in range(4):
             nc.sync.dma_start(out=planes_i[r:P:32, 0 : F // 4], in_=s1_i[r:16:4, :])
-        nc.sync.dma_start(out=w1raw[:, 0:1024].bitcast(I32), in_=w1_i[:, 0:1024])
-        nc.sync.dma_start(out=w1raw[:, 1024:2048].bitcast(I32), in_=w1_i[:, 1024:2048])
-        nc.sync.dma_start(out=x_sb[:, 4:8, :], in_=x_v[:, 4:8, :])
+        nc.sync.dma_start(out=w1[:, 0:1024].bitcast(I32), in_=w1_i[:, 0:1024])
+        nc.sync.dma_start(out=w1[:, 1024:2048].bitcast(I32), in_=w1_i[:, 1024:2048])
+        nc.sync.dma_start(out=x_sb[:, 2:8, :], in_=x_v[:, 2:8, :])
+        nc.sync.dma_start(out=x_sb[:, 8:16, :], in_=x_v[:, 8:16, :])
         for r in range(4):
             nc.sync.dma_start(
                 out=planes_i[r:P:32, F // 4 : F // 2].rearrange("p (g n) -> p g n", g=NG),
                 in_=s2_i[r:16:4, :, :],
             )
         nc.sync.dma_start(out=w2[:].bitcast(I32), in_=w2_i)
-        nc.sync.dma_start(out=x_sb[:, 8:16, :], in_=x_v[:, 8:16, :])
 
-        b1col = keep.tile([P, 16], F32, name="b1col")
+        b1p = keep.tile([P, NG, 4, P], BF16, name="b1p")
         b2bc = keep.tile([P, H], F32, name="b2bc")
-        b2m = keep.tile([P, NT, H], BF16, name="b2m")
+        b2m = keep.tile([P, NT, H], F32, name="b2m")
         mask = keep.tile([P, NT], F32, name="mask")
         xq = keep.tile([P, NT * P], U32, name="xq", align_bytes=64)
         xs = keep.tile([P, NT * P], U8, name="xs", align_bytes=64)
 
-        nc.vector.tensor_single_scalar(out=mask[:], in_=pad_sb[:], scalar=1e-9, op=ALU.is_lt)
-        bt = ps_h.tile([P, P], BF16, name="bt", tag="hb")
-        nc.tensor.transpose(bt[:], brows[:], identb[:])
-        nc.vector.tensor_copy(out=b1col[:], in_=bt[:, 0:16])
-        b2ps = ps_y.tile([P, H], F32, name="b2ps", tag="yb")
-        nc.tensor.matmul(out=b2ps[:], lhsT=ones[:], rhs=brow2[:], start=True, stop=True)
-        nc.scalar.activation(out=b2bc[:], in_=b2ps[:], func=ACT.Copy)
+        def bias_mm(col, tag):
+            ps = psum.tile([P, 512], F32, name="bias_" + tag, tag=tag)
+            nc.tensor.matmul(out=ps[:], lhsT=ones[:], rhs=brow[:, col : col + 512], start=True, stop=True)
+            return ps
 
-        nc.vector.tensor_copy(
-            out=s1[:].bitcast(I32).rearrange("p (g c a) -> p g c a", g=NG, c=4),
-            in_=planes_i[:, 0 : F // 4].rearrange("p (g a c) -> p g c a", g=NG, c=4),
-        )
+        def by_t(ps):
+            return ps[:].rearrange("n (p t) -> n t p", t=4)
 
-        def permute_w1(g):
-            cols = slice(512 * g, 512 * (g + 1))
-            nc.vector.tensor_copy(
-                out=w1[:, cols].bitcast(I32).rearrange("p (c a r) -> p c a r", c=4, r=4),
-                in_=w1raw[:, cols].bitcast(I32).rearrange("p (a c r) -> p c a r", c=4, r=4),
-            )
+        xts = {}
+        xgs = {}
 
-        def x_pair(j, eng):
-            xt = ps_h.tile([P, 2, 2, P], F32, name="xt", tag="hb")
+        def x_transpose(j, tag):
+            xt = psum.tile([P, 2, 2, P], F32, name="xt_" + tag, tag=tag)
             for a in range(2):
                 words = x_sb[:, 2 * j + a, :].bitcast(F32)
                 for u in range(2):
                     nc.tensor.transpose(xt[:, a, u, :], words[:, u : H // 2 : 2], identf[:])
-            xg = ring.tile([P, 2, P, 4], BF16, name="xg", tag="xg", bufs=4, align_bytes=64)
-            src = xt[:].rearrange("p a u n -> p a n u")
+            xts[j] = xt
+
+        def x_evac(j, eng):
+            xg = ring.tile([P, 2, P, 4], BF16, name="xg", tag="xg", bufs=8, align_bytes=64)
+            src = xts[j][:].rearrange("p a u n -> p a n u")
             if eng == "v":
                 nc.vector.tensor_copy(out=xg[:].bitcast(F32), in_=src)
             else:
                 nc.scalar.copy(out=xg[:].bitcast(F32), in_=src)
+            xgs[j] = xg
+
+        def x_quant(j):
             nc.vector.quantize_mx(
                 out=xq[:, 256 * j : 256 * (j + 1)].bitcast(FP8X4),
                 scales=xs[:, 256 * j : 256 * (j + 1)],
-                in_=xg[:].rearrange("p a n t -> p (a n t)"),
+                in_=xgs[j][:].rearrange("p a n t -> p (a n t)"),
             )
 
-        folded = {}
+        hbs = {}
+        hsb = {}
+        tps = {}
+        grps = {}
+        hqs = {}
+        ybs = {}
+        ysb = {}
 
-        def layer1(b):
-            ht = ring.tile([P, 16, TB], BF16, name="ht", tag="ht", bufs=3)
-            rt = ring.tile([P, NG, 4, TB], BF16, name="rt", tag="rt", bufs=2)
-            k = 0
-            for cq in range(4):
-                for g in range(NG):
-                    c = 4 * g + cq
-                    hb = ps_h.tile([P, TB], F32, name="hb", tag="hb")
-                    nc.tensor.matmul_mx(
-                        out=hb[:],
-                        lhsT=w1[:, P * c : P * (c + 1)].bitcast(FP8X4),
-                        lhsT_scale=s1[:, P * c : P * (c + 1)],
-                        rhs=xq[:, TB * b : TB * (b + 1)].bitcast(FP8X4),
-                        rhs_scale=xs[:, TB * b : TB * (b + 1)],
-                        start=True,
-                        stop=True,
-                    )
-                    if k % 2 == 1 and k // 2 < V_SHARE[b]:
-                        nc.vector.tensor_scalar_add(out=ht[:, c, :], in0=hb[:], scalar1=b1col[:, c : c + 1])
-                    else:
-                        nc.scalar.activation(out=ht[:, c, :], in_=hb[:], func=ACT.Identity, bias=b1col[:, c : c + 1])
-                    k += 1
-                for t in range(4):
-                    nc.sync.dma_start(out=rt[cq:P:4, :, t, :], in_=ht[t:P:4, cq:16:4, :])
-            folded[b] = rt
+        def layer1(i):
+            for g in range(NG):
+                hb = psum.tile([P, 512], F32, name="hb%d" % g, tag="hb%d" % g)
+                nc.tensor.matmul_mx(
+                    out=hb[:],
+                    lhsT=xq[:, P * i : P * (i + 1)].bitcast(FP8X4),
+                    lhsT_scale=xs[:, P * i : P * (i + 1)],
+                    rhs=w1[:, 512 * g : 512 * (g + 1)].bitcast(FP8X4),
+                    rhs_scale=planes[:, 512 * g : 512 * (g + 1)],
+                    start=True,
+                    stop=True,
+                )
+                hbs[(i, g)] = hb
+            hsb[i] = ring.tile([P, NG, 4, P], BF16, name="h_sb", tag="h_sb", bufs=3)
+
+        def evac1(i, g):
+            nc.vector.tensor_tensor(out=hsb[i][:, g], in0=by_t(hbs[(i, g)]), in1=b1p[:, g], op=ALU.add)
+
+        def h_transpose(i):
+            for half in range(2):
+                tag = TP_BANKS[(2 * i + half) % 3]
+                tp = psum.tile([P, 2, 4, P], BF16, name="t_" + tag, tag=tag)
+                for gg in range(2):
+                    for t in range(4):
+                        nc.tensor.transpose(tp[:, gg, t, :], hsb[i][:, 2 * half + gg, t, :], identb[:])
+                tps[(i, half)] = tp
+            grps[i] = ring.tile([P, NG, P, 4], BF16, name="grp", tag="grp", bufs=3, align_bytes=64)
+            hqs[i] = (
+                ring.tile([P, NG * P], U32, name="hq", tag="hq", bufs=3, align_bytes=64),
+                ring.tile([P, NG * P], U8, name="hs", tag="hs", bufs=3, align_bytes=64),
+            )
+
+        def evac2(i, half, eng):
+            src = tps[(i, half)][:].rearrange("p g t n -> p g n t")
+            dst = grps[i][:, 2 * half : 2 * half + 2]
+            if eng == "v":
+                nc.vector.tensor_copy(out=dst, in_=src)
+            else:
+                nc.scalar.copy(out=dst, in_=src)
+
+        def h_quant(i):
+            hq, hs = hqs[i]
+            nc.vector.quantize_mx(
+                out=hq[:].bitcast(FP8X4),
+                scales=hs[:],
+                in_=grps[i][:].rearrange("p g n t -> p (g n t)"),
+            )
+
+        def layer2(i):
+            hq, hs = hqs[i]
+            yb = psum.tile([P, H], F32, name="yb", tag="yb")
+            for g in range(NG):
+                nc.tensor.matmul_mx(
+                    out=yb[:],
+                    lhsT=hq[:, P * g : P * (g + 1)].bitcast(FP8X4),
+                    lhsT_scale=hs[:, P * g : P * (g + 1)],
+                    rhs=w2[:, g, :].bitcast(FP8X4),
+                    rhs_scale=planes[:, F + H * g : F + H * (g + 1)],
+                    start=(g == 0),
+                    stop=(g == NG - 1),
+                )
+            ybs[i] = yb
 
         def masked_bias(i):
             nc.gpsimd.tensor_scalar(
@@ -180,65 +210,77 @@ def tile_feedforwardnetwork_kernel(
                 op1=ALU.add,
             )
 
-        def regroup(b, g):
-            grp = ring.tile([P, TB, 4], BF16, name="grp", tag="grp", bufs=3, align_bytes=64)
-            nc.vector.tensor_copy(out=grp[:], in_=folded[b][:, g].rearrange("p t n -> p n t"))
-            return grp
-
-        def layer2(b):
-            hq = ring.tile([P, NG, TB], U32, name="hq", tag="hq", bufs=2, align_bytes=64)
-            hs = ring.tile([P, NG, TB], U8, name="hs", tag="hs", bufs=2, align_bytes=64)
-            ybs = []
-            for ii in range(4):
-                ybs.append(ps_y.tile([P, H], F32, name="yb", tag="yb"))
-            grps = [regroup(b, 0)]
-            for g in range(NG):
-                if g + 1 < NG:
-                    grps.append(regroup(b, g + 1))
-                nc.vector.quantize_mx(
-                    out=hq[:, g, :].bitcast(FP8X4),
-                    scales=hs[:, g, :],
-                    in_=grps[g][:].rearrange("p n t -> p (n t)"),
+        def evac3(i, on_vector):
+            y = ring.tile([P, H], F32, name="y_sb", tag="y_sb", bufs=3)
+            if on_vector:
+                nc.vector.scalar_tensor_tensor(
+                    out=y[:],
+                    in0=ybs[i][:],
+                    scalar=mask[:, i : i + 1],
+                    in1=b2m[:, i, :],
+                    op0=ALU.mult,
+                    op1=ALU.add,
                 )
-                for ii in range(4):
-                    nc.tensor.matmul_mx(
-                        out=ybs[ii][:],
-                        lhsT=hq[:, g, P * ii : P * (ii + 1)].bitcast(FP8X4),
-                        lhsT_scale=hs[:, g, P * ii : P * (ii + 1)],
-                        rhs=w2[:, g, :].bitcast(FP8X4),
-                        rhs_scale=planes[:, F + H * g : F + H * (g + 1)],
-                        start=(g == 0),
-                        stop=(g == NG - 1),
-                    )
-            for ii in range(4):
-                i = 4 * b + ii
-                y = ring.tile([P, H], F32, name="y_sb", tag="y_sb", bufs=4)
-                if i >= E3_ON_VECTOR_FROM:
-                    nc.vector.scalar_tensor_tensor(
-                        out=y[:],
-                        in0=ybs[ii][:],
-                        scalar=mask[:, i : i + 1],
-                        in1=b2m[:, i, :],
-                        op0=ALU.mult,
-                        op1=ALU.add,
-                    )
-                else:
-                    nc.scalar.activation(out=y[:], in_=ybs[ii][:], func=ACT.Copy, scale=mask[:, i : i + 1])
-                    nc.gpsimd.tensor_tensor(out=y[:], in0=y[:], in1=b2m[:, i, :], op=ALU.add)
-                nc.sync.dma_start(out=out_v[:, i, :], in_=y[:])
+            else:
+                nc.scalar.activation(out=y[:], in_=ybs[i][:], func=ACT.Copy, scale=mask[:, i : i + 1])
+                nc.gpsimd.tensor_tensor(out=y[:], in0=y[:], in1=b2m[:, i, :], op=ALU.add)
+            nc.sync.dma_start(out=out_v[:, i, :], in_=y[:])
 
-        permute_w1(0)
-        x_pair(0, "v")
-        x_pair(1, "s")
-        for g in range(1, NG):
-            permute_w1(g)
-        for i in range(NT):
-            masked_bias(i)
-        for b in range(NB):
-            layer1(b)
-            if b + 1 < NB:
-                x_pair(2 * b + 2, "s")
-                x_pair(2 * b + 3, "s")
-            if b >= 1:
-                layer2(b - 1)
-        layer2(NB - 1)
+        ps0 = bias_mm(0, "yb")
+        ps1 = bias_mm(512, "xb")
+        nc.vector.tensor_copy(out=b1p[:, 0], in_=by_t(ps0))
+        nc.scalar.copy(out=b1p[:, 1], in_=by_t(ps1))
+        nc.vector.tensor_single_scalar(out=mask[:], in_=pad_sb[:], scalar=1e-9, op=ALU.is_lt)
+        x_transpose(0, "hb0")
+        x_transpose(1, "hb1")
+        x_evac(0, "v")
+        x_evac(1, "s")
+        x_quant(0)
+        ps2 = bias_mm(1024, "tp0")
+        ps3 = bias_mm(1536, "tp1")
+        ps4 = bias_mm(2048, "yb")
+        nc.scalar.copy(out=b1p[:, 2], in_=by_t(ps2))
+        nc.scalar.copy(out=b1p[:, 3], in_=by_t(ps3))
+        nc.scalar.activation(out=b2bc[:], in_=ps4[:], func=ACT.Copy)
+
+        layer1(0)
+        evac1(0, 0)
+        evac1(0, 1)
+        x_quant(1)
+        evac1(0, 2)
+        evac1(0, 3)
+        x_transpose(2, "tp0")
+        x_transpose(3, "tp1")
+        x_evac(2, "s")
+        x_evac(3, "s")
+
+        for c in range(NT + 2):
+            if 0 <= c - 2 < NT:
+                layer2(c - 2)
+            if c + 1 < NT:
+                layer1(c + 1)
+                for g in range(NG):
+                    evac1(c + 1, g)
+                if c <= 2:
+                    x_quant(2 * c + 2)
+                    x_quant(2 * c + 3)
+            if 0 <= c - 1 < NT:
+                evac2(c - 1, 0, "s")
+            if 0 <= c - 2 < NT:
+                evac3(c - 2, c - 2 == NT - 1)
+            if 0 <= c - 1 < NT:
+                evac2(c - 1, 1, "v" if c - 1 == NT - 1 else "s")
+                h_quant(c - 1)
+            if c < NT:
+                h_transpose(c)
+                masked_bias(c)
+            if c == 0:
+                x_transpose(4, "xb")
+                x_transpose(5, "yb")
+                x_evac(4, "s")
+                x_evac(5, "s")
+            if c == 1:
+                x_transpose(6, "yb")
+                x_evac(6, "s")
+                x_transpose(7, "yb")
+                x_evac(7, "s")

@@ -19,7 +19,6 @@ NT = 16
 H = 512
 F = 2048
 NG = 4
-TP_BANKS = ("tp0", "tp1", "xb")
 
 
 def tile_feedforwardnetwork_kernel(
@@ -57,8 +56,6 @@ def tile_feedforwardnetwork_kernel(
         nc.scalar.dma_start(out=brow[0:1, 0:F], in_=filter_bias.rearrange("(o f) -> o f", o=1))
         nc.scalar.dma_start(out=brow[0:1, F : F + H], in_=output_bias.rearrange("(o f) -> o f", o=1))
         nc.scalar.dma_start(out=pad_sb[:], in_=pad_v)
-        warm = keep.tile([P, 1], F32, name="warm")
-        nc.scalar.activation(out=warm[:], in_=ones[:, 0:1], func=ACT.Copy)
 
         identf = keep.tile([P, P], F32, name="identf")
         identb = keep.tile([P, P], BF16, name="identb")
@@ -79,15 +76,15 @@ def tile_feedforwardnetwork_kernel(
         nc.sync.dma_start(out=w1[:, 0:1024].bitcast(I32), in_=w1_i[:, 0:1024])
         nc.sync.dma_start(out=w1[:, 1024:2048].bitcast(I32), in_=w1_i[:, 1024:2048])
         nc.sync.dma_start(out=x_sb[:, 2:8, :], in_=x_v[:, 2:8, :])
-        nc.sync.dma_start(out=x_sb[:, 8:16, :], in_=x_v[:, 8:16, :])
         for r in range(4):
             nc.sync.dma_start(
                 out=planes_i[r:P:32, F // 4 : F // 2].rearrange("p (g n) -> p g n", g=NG),
                 in_=s2_i[r:16:4, :, :],
             )
         nc.sync.dma_start(out=w2[:].bitcast(I32), in_=w2_i)
+        nc.sync.dma_start(out=x_sb[:, 8:16, :], in_=x_v[:, 8:16, :])
 
-        b1p = keep.tile([P, NG, 4, P], BF16, name="b1p")
+        b1p = keep.tile([P, NG, P, 4], BF16, name="b1p")
         b2bc = keep.tile([P, H], F32, name="b2bc")
         b2m = keep.tile([P, NT, H], F32, name="b2m")
         mask = keep.tile([P, NT], F32, name="mask")
@@ -100,7 +97,7 @@ def tile_feedforwardnetwork_kernel(
             return ps
 
         def by_t(ps):
-            return ps[:].rearrange("n (p t) -> n t p", t=4)
+            return ps[:].rearrange("n (p t) -> n p t", t=4)
 
         xts = {}
         xgs = {}
@@ -114,7 +111,7 @@ def tile_feedforwardnetwork_kernel(
             xts[j] = xt
 
         def x_evac(j, eng):
-            xg = ring.tile([P, 2, P, 4], BF16, name="xg", tag="xg", bufs=8, align_bytes=64)
+            xg = ring.tile([P, 2, P, 4], BF16, name="xg", tag="xg", bufs=3, align_bytes=64)
             src = xts[j][:].rearrange("p a u n -> p a n u")
             if eng == "v":
                 nc.vector.tensor_copy(out=xg[:].bitcast(F32), in_=src)
@@ -153,12 +150,16 @@ def tile_feedforwardnetwork_kernel(
             hsb[i] = ring.tile([P, NG, 4, P], BF16, name="h_sb", tag="h_sb", bufs=3)
 
         def evac1(i, g):
-            nc.vector.tensor_tensor(out=hsb[i][:, g], in0=by_t(hbs[(i, g)]), in1=b1p[:, g], op=ALU.add)
+            nc.vector.tensor_tensor(
+                out=hsb[i][:, g].rearrange("n t p -> n p t"),
+                in0=hbs[(i, g)][:].rearrange("n (p t) -> n p t", t=4),
+                in1=b1p[:, g],
+                op=ALU.add,
+            )
 
         def h_transpose(i):
             for half in range(2):
-                tag = TP_BANKS[(2 * i + half) % 3]
-                tp = psum.tile([P, 2, 4, P], BF16, name="t_" + tag, tag=tag)
+                tp = psum.tile([P, 2, 4, P], BF16, name="tp%d" % half, tag="tp%d" % half)
                 for gg in range(2):
                     for t in range(4):
                         nc.tensor.transpose(tp[:, gg, t, :], hsb[i][:, 2 * half + gg, t, :], identb[:])
@@ -177,12 +178,12 @@ def tile_feedforwardnetwork_kernel(
             else:
                 nc.scalar.copy(out=dst, in_=src)
 
-        def h_quant(i):
+        def h_quant(i, half):
             hq, hs = hqs[i]
             nc.vector.quantize_mx(
-                out=hq[:].bitcast(FP8X4),
-                scales=hs[:],
-                in_=grps[i][:].rearrange("p g n t -> p (g n t)"),
+                out=hq[:, 256 * half : 256 * (half + 1)].bitcast(FP8X4),
+                scales=hs[:, 256 * half : 256 * (half + 1)],
+                in_=grps[i][:, 2 * half : 2 * half + 2].rearrange("p g n t -> p (g n t)"),
             )
 
         def layer2(i):
@@ -238,10 +239,12 @@ def tile_feedforwardnetwork_kernel(
         x_quant(0)
         ps2 = bias_mm(1024, "tp0")
         ps3 = bias_mm(1536, "tp1")
-        ps4 = bias_mm(2048, "yb")
+        ps4 = bias_mm(2048, "hb2")
         nc.scalar.copy(out=b1p[:, 2], in_=by_t(ps2))
         nc.scalar.copy(out=b1p[:, 3], in_=by_t(ps3))
         nc.scalar.activation(out=b2bc[:], in_=ps4[:], func=ACT.Copy)
+        masked_bias(0)
+        masked_bias(1)
 
         layer1(0)
         evac1(0, 0)
@@ -249,38 +252,38 @@ def tile_feedforwardnetwork_kernel(
         x_quant(1)
         evac1(0, 2)
         evac1(0, 3)
-        x_transpose(2, "tp0")
-        x_transpose(3, "tp1")
+        x_transpose(2, "xb")
+        x_transpose(3, "yb")
         x_evac(2, "s")
         x_evac(3, "s")
 
-        for c in range(NT + 2):
-            if 0 <= c - 2 < NT:
-                layer2(c - 2)
-            if c + 1 < NT:
-                layer1(c + 1)
-                for g in range(NG):
-                    evac1(c + 1, g)
-                if c <= 2:
-                    x_quant(2 * c + 2)
-                    x_quant(2 * c + 3)
-            if 0 <= c - 1 < NT:
-                evac2(c - 1, 0, "s")
-            if 0 <= c - 2 < NT:
-                evac3(c - 2, c - 2 == NT - 1)
-            if 0 <= c - 1 < NT:
-                evac2(c - 1, 1, "v" if c - 1 == NT - 1 else "s")
-                h_quant(c - 1)
-            if c < NT:
-                h_transpose(c)
-                masked_bias(c)
-            if c == 0:
-                x_transpose(4, "xb")
-                x_transpose(5, "yb")
-                x_evac(4, "s")
-                x_evac(5, "s")
-            if c == 1:
-                x_transpose(6, "yb")
-                x_evac(6, "s")
-                x_transpose(7, "yb")
-                x_evac(7, "s")
+        for s in range(NT + 1):
+            if s >= 1:
+                h_quant(s - 1, 0)
+            if s + 1 < NT:
+                layer1(s + 1)
+                evac1(s + 1, 0)
+            if s >= 1:
+                h_quant(s - 1, 1)
+            if s + 1 < NT:
+                evac1(s + 1, 1)
+                if s == 0:
+                    x_quant(2)
+                    x_quant(3)
+                if 1 <= s <= 4:
+                    x_quant(s + 3)
+                evac1(s + 1, 2)
+                evac1(s + 1, 3)
+            if s < NT:
+                h_transpose(s)
+                last = s == NT - 1
+                evac2(s, 0, "s")
+                evac2(s, 1, "v" if last else "s")
+            if s <= 3:
+                x_transpose(s + 4, "xb")
+                x_evac(s + 4, "s")
+            if s >= 1:
+                layer2(s - 1)
+                evac3(s - 1, s - 1 == NT - 1)
+            if s + 2 < NT:
+                masked_bias(s + 2)

@@ -19,6 +19,7 @@ NT = 16
 H = 512
 F = 2048
 NG = 4
+TP_BANKS = ("tp0", "tp1", "xb")
 
 
 def tile_feedforwardnetwork_kernel(
@@ -56,6 +57,8 @@ def tile_feedforwardnetwork_kernel(
         nc.scalar.dma_start(out=brow[0:1, 0:F], in_=filter_bias.rearrange("(o f) -> o f", o=1))
         nc.scalar.dma_start(out=brow[0:1, F : F + H], in_=output_bias.rearrange("(o f) -> o f", o=1))
         nc.scalar.dma_start(out=pad_sb[:], in_=pad_v)
+        warm = keep.tile([P, 1], F32, name="warm")
+        nc.scalar.activation(out=warm[:], in_=ones[:, 0:1], func=ACT.Copy)
 
         identf = keep.tile([P, P], F32, name="identf")
         identb = keep.tile([P, P], BF16, name="identb")
@@ -76,15 +79,15 @@ def tile_feedforwardnetwork_kernel(
         nc.sync.dma_start(out=w1[:, 0:1024].bitcast(I32), in_=w1_i[:, 0:1024])
         nc.sync.dma_start(out=w1[:, 1024:2048].bitcast(I32), in_=w1_i[:, 1024:2048])
         nc.sync.dma_start(out=x_sb[:, 2:8, :], in_=x_v[:, 2:8, :])
+        nc.sync.dma_start(out=x_sb[:, 8:16, :], in_=x_v[:, 8:16, :])
         for r in range(4):
             nc.sync.dma_start(
                 out=planes_i[r:P:32, F // 4 : F // 2].rearrange("p (g n) -> p g n", g=NG),
                 in_=s2_i[r:16:4, :, :],
             )
         nc.sync.dma_start(out=w2[:].bitcast(I32), in_=w2_i)
-        nc.sync.dma_start(out=x_sb[:, 8:16, :], in_=x_v[:, 8:16, :])
 
-        b1p = keep.tile([P, NG, P, 4], BF16, name="b1p")
+        b1p = keep.tile([P, NG, 4, P], BF16, name="b1p")
         b2bc = keep.tile([P, H], F32, name="b2bc")
         b2m = keep.tile([P, NT, H], F32, name="b2m")
         mask = keep.tile([P, NT], F32, name="mask")
@@ -97,7 +100,7 @@ def tile_feedforwardnetwork_kernel(
             return ps
 
         def by_t(ps):
-            return ps[:].rearrange("n (p t) -> n p t", t=4)
+            return ps[:].rearrange("n (p t) -> n t p", t=4)
 
         xts = {}
         xgs = {}
@@ -111,7 +114,7 @@ def tile_feedforwardnetwork_kernel(
             xts[j] = xt
 
         def x_evac(j, eng):
-            xg = ring.tile([P, 2, P, 4], BF16, name="xg", tag="xg", bufs=3, align_bytes=64)
+            xg = ring.tile([P, 2, P, 4], BF16, name="xg", tag="xg", bufs=8, align_bytes=64)
             src = xts[j][:].rearrange("p a u n -> p a n u")
             if eng == "v":
                 nc.vector.tensor_copy(out=xg[:].bitcast(F32), in_=src)
@@ -150,16 +153,12 @@ def tile_feedforwardnetwork_kernel(
             hsb[i] = ring.tile([P, NG, 4, P], BF16, name="h_sb", tag="h_sb", bufs=3)
 
         def evac1(i, g):
-            nc.vector.tensor_tensor(
-                out=hsb[i][:, g].rearrange("n t p -> n p t"),
-                in0=hbs[(i, g)][:].rearrange("n (p t) -> n p t", t=4),
-                in1=b1p[:, g],
-                op=ALU.add,
-            )
+            nc.vector.tensor_tensor(out=hsb[i][:, g], in0=by_t(hbs[(i, g)]), in1=b1p[:, g], op=ALU.add)
 
         def h_transpose(i):
             for half in range(2):
-                tp = psum.tile([P, 2, 4, P], BF16, name="tp%d" % half, tag="tp%d" % half)
+                tag = TP_BANKS[(2 * i + half) % 3]
+                tp = psum.tile([P, 2, 4, P], BF16, name="t_" + tag, tag=tag)
                 for gg in range(2):
                     for t in range(4):
                         nc.tensor.transpose(tp[:, gg, t, :], hsb[i][:, 2 * half + gg, t, :], identb[:])
@@ -178,12 +177,12 @@ def tile_feedforwardnetwork_kernel(
             else:
                 nc.scalar.copy(out=dst, in_=src)
 
-        def h_quant(i, half):
+        def h_quant(i, g0, g1):
             hq, hs = hqs[i]
             nc.vector.quantize_mx(
-                out=hq[:, 256 * half : 256 * (half + 1)].bitcast(FP8X4),
-                scales=hs[:, 256 * half : 256 * (half + 1)],
-                in_=grps[i][:, 2 * half : 2 * half + 2].rearrange("p g n t -> p (g n t)"),
+                out=hq[:, P * g0 : P * g1].bitcast(FP8X4),
+                scales=hs[:, P * g0 : P * g1],
+                in_=grps[i][:, g0:g1].rearrange("p g n t -> p (g n t)"),
             )
 
         def layer2(i):
@@ -239,12 +238,10 @@ def tile_feedforwardnetwork_kernel(
         x_quant(0)
         ps2 = bias_mm(1024, "tp0")
         ps3 = bias_mm(1536, "tp1")
-        ps4 = bias_mm(2048, "hb2")
+        ps4 = bias_mm(2048, "yb")
         nc.scalar.copy(out=b1p[:, 2], in_=by_t(ps2))
         nc.scalar.copy(out=b1p[:, 3], in_=by_t(ps3))
         nc.scalar.activation(out=b2bc[:], in_=ps4[:], func=ACT.Copy)
-        masked_bias(0)
-        masked_bias(1)
 
         layer1(0)
         evac1(0, 0)
@@ -252,38 +249,43 @@ def tile_feedforwardnetwork_kernel(
         x_quant(1)
         evac1(0, 2)
         evac1(0, 3)
-        x_transpose(2, "xb")
-        x_transpose(3, "yb")
+        x_transpose(2, "tp0")
+        x_transpose(3, "tp1")
         x_evac(2, "s")
         x_evac(3, "s")
 
-        for s in range(NT + 1):
-            if s >= 1:
-                h_quant(s - 1, 0)
-            if s + 1 < NT:
-                layer1(s + 1)
-                evac1(s + 1, 0)
-            if s >= 1:
-                h_quant(s - 1, 1)
-            if s + 1 < NT:
-                evac1(s + 1, 1)
-                if s == 0:
-                    x_quant(2)
-                    x_quant(3)
-                if 1 <= s <= 4:
-                    x_quant(s + 3)
-                evac1(s + 1, 2)
-                evac1(s + 1, 3)
-            if s < NT:
-                h_transpose(s)
-                last = s == NT - 1
-                evac2(s, 0, "s")
-                evac2(s, 1, "v" if last else "s")
-            if s <= 3:
-                x_transpose(s + 4, "xb")
-                x_evac(s + 4, "s")
-            if s >= 1:
-                layer2(s - 1)
-                evac3(s - 1, s - 1 == NT - 1)
-            if s + 2 < NT:
-                masked_bias(s + 2)
+        for c in range(NT + 2):
+            if c + 1 < NT:
+                layer1(c + 1)
+                for g in range(NG):
+                    evac1(c + 1, g)
+                if c <= 2:
+                    x_quant(2 * c + 2)
+                    x_quant(2 * c + 3)
+            if 0 <= c - 2 < NT:
+                layer2(c - 2)
+            if 0 <= c - 1 < NT:
+                if c - 1 == NT - 1:
+                    evac2(c - 1, 1, "v")
+                    evac2(c - 1, 0, "s")
+                    h_quant(c - 1, 0, 2)
+                    h_quant(c - 1, 2, 4)
+                else:
+                    evac2(c - 1, 0, "s")
+                    evac2(c - 1, 1, "s")
+                    h_quant(c - 1, 0, 4)
+            if 0 <= c - 2 < NT:
+                evac3(c - 2, c - 2 == NT - 1)
+            if c < NT:
+                h_transpose(c)
+                masked_bias(c)
+            if c == 0:
+                x_transpose(4, "xb")
+                x_transpose(5, "yb")
+                x_evac(4, "s")
+                x_evac(5, "s")
+            if c == 1:
+                x_transpose(6, "yb")
+                x_evac(6, "s")
+                x_transpose(7, "yb")
+                x_evac(7, "s")

@@ -19,7 +19,6 @@ NT = 16
 H = 512
 F = 2048
 NG = 4
-TP_BANKS = ("tp0", "tp1", "xb")
 
 
 def tile_feedforwardnetwork_kernel(
@@ -36,7 +35,6 @@ def tile_feedforwardnetwork_kernel(
 ):
     nc = tc.nc
     with ExitStack() as ctx:
-        ctx.enter_context(tc.manual_schedule())
         keep = ctx.enter_context(tc.tile_pool(name="keep", bufs=1))
         ring = ctx.enter_context(tc.tile_pool(name="ring", bufs=2))
         psum = ctx.enter_context(tc.psum_pool(name="psum", bufs=1))
@@ -57,8 +55,6 @@ def tile_feedforwardnetwork_kernel(
         nc.scalar.dma_start(out=brow[0:1, 0:F], in_=filter_bias.rearrange("(o f) -> o f", o=1))
         nc.scalar.dma_start(out=brow[0:1, F : F + H], in_=output_bias.rearrange("(o f) -> o f", o=1))
         nc.scalar.dma_start(out=pad_sb[:], in_=pad_v)
-        warm = keep.tile([P, 1], F32, name="warm")
-        nc.scalar.activation(out=warm[:], in_=ones[:, 0:1], func=ACT.Copy)
 
         identf = keep.tile([P, P], F32, name="identf")
         identb = keep.tile([P, P], BF16, name="identb")
@@ -79,13 +75,13 @@ def tile_feedforwardnetwork_kernel(
         nc.sync.dma_start(out=w1[:, 0:1024].bitcast(I32), in_=w1_i[:, 0:1024])
         nc.sync.dma_start(out=w1[:, 1024:2048].bitcast(I32), in_=w1_i[:, 1024:2048])
         nc.sync.dma_start(out=x_sb[:, 2:8, :], in_=x_v[:, 2:8, :])
-        nc.sync.dma_start(out=x_sb[:, 8:16, :], in_=x_v[:, 8:16, :])
         for r in range(4):
             nc.sync.dma_start(
                 out=planes_i[r:P:32, F // 4 : F // 2].rearrange("p (g n) -> p g n", g=NG),
                 in_=s2_i[r:16:4, :, :],
             )
         nc.sync.dma_start(out=w2[:].bitcast(I32), in_=w2_i)
+        nc.sync.dma_start(out=x_sb[:, 8:16, :], in_=x_v[:, 8:16, :])
 
         b1p = keep.tile([P, NG, 4, P], BF16, name="b1p")
         b2bc = keep.tile([P, H], F32, name="b2bc")
@@ -114,7 +110,7 @@ def tile_feedforwardnetwork_kernel(
             xts[j] = xt
 
         def x_evac(j, eng):
-            xg = ring.tile([P, 2, P, 4], BF16, name="xg", tag="xg", bufs=8, align_bytes=64)
+            xg = ring.tile([P, 2, P, 4], BF16, name="xg", tag="xg", bufs=3, align_bytes=64)
             src = xts[j][:].rearrange("p a u n -> p a n u")
             if eng == "v":
                 nc.vector.tensor_copy(out=xg[:].bitcast(F32), in_=src)
@@ -157,8 +153,7 @@ def tile_feedforwardnetwork_kernel(
 
         def h_transpose(i):
             for half in range(2):
-                tag = TP_BANKS[(2 * i + half) % 3]
-                tp = psum.tile([P, 2, 4, P], BF16, name="t_" + tag, tag=tag)
+                tp = psum.tile([P, 2, 4, P], BF16, name="tp%d" % half, tag="tp%d" % half)
                 for gg in range(2):
                     for t in range(4):
                         nc.tensor.transpose(tp[:, gg, t, :], hsb[i][:, 2 * half + gg, t, :], identb[:])
@@ -177,12 +172,12 @@ def tile_feedforwardnetwork_kernel(
             else:
                 nc.scalar.copy(out=dst, in_=src)
 
-        def h_quant(i, g0, g1):
+        def h_quant(i, half):
             hq, hs = hqs[i]
             nc.vector.quantize_mx(
-                out=hq[:, P * g0 : P * g1].bitcast(FP8X4),
-                scales=hs[:, P * g0 : P * g1],
-                in_=grps[i][:, g0:g1].rearrange("p g n t -> p (g n t)"),
+                out=hq[:, 256 * half : 256 * (half + 1)].bitcast(FP8X4),
+                scales=hs[:, 256 * half : 256 * (half + 1)],
+                in_=grps[i][:, 2 * half : 2 * half + 2].rearrange("p g n t -> p (g n t)"),
             )
 
         def layer2(i):
@@ -238,10 +233,12 @@ def tile_feedforwardnetwork_kernel(
         x_quant(0)
         ps2 = bias_mm(1024, "tp0")
         ps3 = bias_mm(1536, "tp1")
-        ps4 = bias_mm(2048, "yb")
+        ps4 = bias_mm(2048, "hb2")
         nc.scalar.copy(out=b1p[:, 2], in_=by_t(ps2))
         nc.scalar.copy(out=b1p[:, 3], in_=by_t(ps3))
         nc.scalar.activation(out=b2bc[:], in_=ps4[:], func=ACT.Copy)
+        masked_bias(0)
+        masked_bias(1)
 
         layer1(0)
         evac1(0, 0)
@@ -249,43 +246,38 @@ def tile_feedforwardnetwork_kernel(
         x_quant(1)
         evac1(0, 2)
         evac1(0, 3)
-        x_transpose(2, "tp0")
-        x_transpose(3, "tp1")
+        x_transpose(2, "xb")
+        x_transpose(3, "yb")
         x_evac(2, "s")
         x_evac(3, "s")
 
-        for c in range(NT + 2):
-            if c + 1 < NT:
-                layer1(c + 1)
-                for g in range(NG):
-                    evac1(c + 1, g)
-                if c <= 2:
-                    x_quant(2 * c + 2)
-                    x_quant(2 * c + 3)
-            if 0 <= c - 2 < NT:
-                layer2(c - 2)
-            if 0 <= c - 1 < NT:
-                if c - 1 == NT - 1:
-                    evac2(c - 1, 1, "v")
-                    evac2(c - 1, 0, "s")
-                    h_quant(c - 1, 0, 2)
-                    h_quant(c - 1, 2, 4)
-                else:
-                    evac2(c - 1, 0, "s")
-                    evac2(c - 1, 1, "s")
-                    h_quant(c - 1, 0, 4)
-            if 0 <= c - 2 < NT:
-                evac3(c - 2, c - 2 == NT - 1)
-            if c < NT:
-                h_transpose(c)
-                masked_bias(c)
-            if c == 0:
-                x_transpose(4, "xb")
-                x_transpose(5, "yb")
-                x_evac(4, "s")
-                x_evac(5, "s")
-            if c == 1:
-                x_transpose(6, "yb")
-                x_evac(6, "s")
-                x_transpose(7, "yb")
-                x_evac(7, "s")
+        for s in range(NT + 1):
+            if s >= 1:
+                h_quant(s - 1, 0)
+            if s + 1 < NT:
+                layer1(s + 1)
+                evac1(s + 1, 0)
+            if s >= 1:
+                h_quant(s - 1, 1)
+            if s + 1 < NT:
+                evac1(s + 1, 1)
+                if s == 0:
+                    x_quant(2)
+                    x_quant(3)
+                if 1 <= s <= 4:
+                    x_quant(s + 3)
+                evac1(s + 1, 2)
+                evac1(s + 1, 3)
+            if s < NT:
+                h_transpose(s)
+                last = s == NT - 1
+                evac2(s, 0, "s")
+                evac2(s, 1, "v" if last else "s")
+            if s <= 3:
+                x_transpose(s + 4, "xb")
+                x_evac(s + 4, "s")
+            if s >= 1:
+                layer2(s - 1)
+                evac3(s - 1, s - 1 == NT - 1)
+            if s + 2 < NT:
+                masked_bias(s + 2)

@@ -35,6 +35,7 @@ def tile_feedforwardnetwork_kernel(
 ):
     nc = tc.nc
     with ExitStack() as ctx:
+        ctx.enter_context(tc.manual_schedule())
         keep = ctx.enter_context(tc.tile_pool(name="keep", bufs=1))
         ring = ctx.enter_context(tc.tile_pool(name="ring", bufs=2))
         psum = ctx.enter_context(tc.psum_pool(name="psum", bufs=1))
@@ -57,9 +58,7 @@ def tile_feedforwardnetwork_kernel(
         nc.scalar.dma_start(out=pad_sb[:], in_=pad_v)
 
         identf = keep.tile([P, P], F32, name="identf")
-        identb = keep.tile([P, P], BF16, name="identb")
         make_identity(nc, identf[:])
-        make_identity(nc, identb[:])
 
         x_sb = keep.tile([P, NT, H], BF16, name="x_sb")
         w1 = keep.tile([P, F], U32, name="w1", align_bytes=64)
@@ -83,7 +82,7 @@ def tile_feedforwardnetwork_kernel(
         nc.sync.dma_start(out=w2[:].bitcast(I32), in_=w2_i)
         nc.sync.dma_start(out=x_sb[:, 8:16, :], in_=x_v[:, 8:16, :])
 
-        b1p = keep.tile([P, NG, 4, P], BF16, name="b1p")
+        b1p = keep.tile([P, NG, 2, P, 2], BF16, name="b1p")
         b2bc = keep.tile([P, H], F32, name="b2bc")
         b2m = keep.tile([P, NT, H], F32, name="b2m")
         mask = keep.tile([P, NT], F32, name="mask")
@@ -96,7 +95,7 @@ def tile_feedforwardnetwork_kernel(
             return ps
 
         def by_t(ps):
-            return ps[:].rearrange("n (p t) -> n t p", t=4)
+            return ps[:].rearrange("n (p u e) -> n u p e", u=2, e=2)
 
         xts = {}
         xgs = {}
@@ -146,17 +145,18 @@ def tile_feedforwardnetwork_kernel(
                     stop=True,
                 )
                 hbs[(i, g)] = hb
-            hsb[i] = ring.tile([P, NG, 4, P], BF16, name="h_sb", tag="h_sb", bufs=3)
+            hsb[i] = ring.tile([P, NG, 2, P, 2], BF16, name="h_sb", tag="h_sb", bufs=3)
 
         def evac1(i, g):
             nc.vector.tensor_tensor(out=hsb[i][:, g], in0=by_t(hbs[(i, g)]), in1=b1p[:, g], op=ALU.add)
 
         def h_transpose(i):
             for half in range(2):
-                tp = psum.tile([P, 2, 4, P], BF16, name="tp%d" % half, tag="tp%d" % half)
+                tp = psum.tile([P, 2, 2, P], F32, name="tp%d" % half, tag="tp%d" % half)
                 for gg in range(2):
-                    for t in range(4):
-                        nc.tensor.transpose(tp[:, gg, t, :], hsb[i][:, 2 * half + gg, t, :], identb[:])
+                    for u in range(2):
+                        words = hsb[i][:, 2 * half + gg, u].rearrange("n p e -> n (p e)").bitcast(F32)
+                        nc.tensor.transpose(tp[:, gg, u, :], words, identf[:])
                 tps[(i, half)] = tp
             grps[i] = ring.tile([P, NG, P, 4], BF16, name="grp", tag="grp", bufs=3, align_bytes=64)
             hqs[i] = (
@@ -165,8 +165,8 @@ def tile_feedforwardnetwork_kernel(
             )
 
         def evac2(i, half, eng):
-            src = tps[(i, half)][:].rearrange("p g t n -> p g n t")
-            dst = grps[i][:, 2 * half : 2 * half + 2]
+            src = tps[(i, half)][:].rearrange("p g u n -> p g n u")
+            dst = grps[i][:, 2 * half : 2 * half + 2].bitcast(F32)
             if eng == "v":
                 nc.vector.tensor_copy(out=dst, in_=src)
             else:

from contextlib import ExitStack

import concourse.mybir as mybir
from concourse.masks import make_identity

FLOPS = 2 * 2048 * 512 * 2048 * 2

F32 = mybir.dt.float32
BF16 = mybir.dt.bfloat16
I32 = mybir.dt.int32
U32 = mybir.dt.uint32
U8 = mybir.dt.uint8
FP8X4 = mybir.dt.float8_e4m3fn_x4
ALU = mybir.AluOpType
ACT = mybir.ActivationFunctionType

P = 128
NT = 16
H = 512
F = 2048
NG = 4


def tile_feedforwardnetwork_kernel(
    tc,
    x,
    padding,
    filter_weight_words,
    filter_weight_scales,
    filter_bias,
    output_weight_words,
    output_weight_scales,
    output_bias,
    out,
):
    nc = tc.nc
    with ExitStack() as ctx:
        ctx.enter_context(tc.manual_schedule())
        keep = ctx.enter_context(tc.tile_pool(name="keep", bufs=1))
        ring = ctx.enter_context(tc.tile_pool(name="ring", bufs=2))
        psum = ctx.enter_context(tc.psum_pool(name="psum", bufs=1))

        x_v = x.rearrange("b (q i) h -> (b q) i h", i=NT)
        out_v = out.rearrange("b (q i) h -> (b q) i h", i=NT)
        pad_v = padding.rearrange("b (q i) -> (b q) i", i=NT)

        brow = keep.tile([P, F + H], BF16, name="brow")
        ones = keep.tile([P, P], BF16, name="ones")
        planes = keep.tile([P, 2 * F], U8, name="planes", align_bytes=64)
        planes_i = planes[:].bitcast(I32)
        nc.vector.memset(brow[:], 0.0)
        nc.vector.memset(ones[:], 1.0)
        nc.vector.memset(planes_i, 0)

        pad_sb = keep.tile([P, NT], BF16, name="pad_sb")
        nc.scalar.dma_start(out=brow[0:1, 0:F], in_=filter_bias.rearrange("(o f) -> o f", o=1))
        nc.scalar.dma_start(out=brow[0:1, F : F + H], in_=output_bias.rearrange("(o f) -> o f", o=1))
        nc.scalar.dma_start(out=pad_sb[:], in_=pad_v)

        identf = keep.tile([P, P], F32, name="identf")
        make_identity(nc, identf[:])

        x_sb = keep.tile([P, NT, H], BF16, name="x_sb")
        w1 = keep.tile([P, F], U32, name="w1", align_bytes=64)
        w2 = keep.tile([P, NG, H], U32, name="w2", align_bytes=64)
        s1_i = filter_weight_scales.rearrange("o q n -> (o q) n").bitcast(I32)
        s2_i = output_weight_scales.rearrange("g q n -> q g n").bitcast(I32)
        w1_i = filter_weight_words.rearrange("o p n t -> (o p) (n t)").bitcast(I32)
        w2_i = output_weight_words.rearrange("g p n t -> p g (n t)").bitcast(I32)

        nc.sync.dma_start(out=x_sb[:, 0:2, :], in_=x_v[:, 0:2, :])
        for r in range(4):
            nc.sync.dma_start(out=planes_i[r:P:32, 0 : F // 4], in_=s1_i[r:16:4, :])
        nc.sync.dma_start(out=w1[:, 0:1024].bitcast(I32), in_=w1_i[:, 0:1024])
        nc.sync.dma_start(out=w1[:, 1024:2048].bitcast(I32), in_=w1_i[:, 1024:2048])
        nc.sync.dma_start(out=x_sb[:, 2:8, :], in_=x_v[:, 2:8, :])
        for r in range(4):
            nc.sync.dma_start(
                out=planes_i[r:P:32, F // 4 : F // 2].rearrange("p (g n) -> p g n", g=NG),
                in_=s2_i[r:16:4, :, :],
            )
        nc.sync.dma_start(out=w2[:].bitcast(I32), in_=w2_i)
        nc.sync.dma_start(out=x_sb[:, 8:16, :], in_=x_v[:, 8:16, :])

        b1p = keep.tile([P, NG, 2, P, 2], BF16, name="b1p")
        b2bc = keep.tile([P, H], F32, name="b2bc")
        b2m = keep.tile([P, NT, H], F32, name="b2m")
        mask = keep.tile([P, NT], F32, name="mask")
        xq = keep.tile([P, NT * P], U32, name="xq", align_bytes=64)
        xs = keep.tile([P, NT * P], U8, name="xs", align_bytes=64)

        def bias_mm(col, tag):
            ps = psum.tile([P, 512], F32, name="bias_" + tag, tag=tag)
            nc.tensor.matmul(out=ps[:], lhsT=ones[:], rhs=brow[:, col : col + 512], start=True, stop=True)
            return ps

        def by_t(ps):
            return ps[:].rearrange("n (p u e) -> n u p e", u=2, e=2)

        xts = {}
        xgs = {}

        def x_transpose(j, tag):
            xt = psum.tile([P, 2, 2, P], F32, name="xt_" + tag, tag=tag)
            for a in range(2):
                words = x_sb[:, 2 * j + a, :].bitcast(F32)
                for u in range(2):
                    nc.tensor.transpose(xt[:, a, u, :], words[:, u : H // 2 : 2], identf[:])
            xts[j] = xt

        def x_evac(j, eng):
            xg = ring.tile([P, 2, P, 4], BF16, name="xg", tag="xg", bufs=3, align_bytes=64)
            src = xts[j][:].rearrange("p a u n -> p a n u")
            if eng == "v":
                nc.vector.tensor_copy(out=xg[:].bitcast(F32), in_=src)
            else:
                nc.scalar.copy(out=xg[:].bitcast(F32), in_=src)
            xgs[j] = xg

        def x_quant(j):
            nc.vector.quantize_mx(
                out=xq[:, 256 * j : 256 * (j + 1)].bitcast(FP8X4),
                scales=xs[:, 256 * j : 256 * (j + 1)],
                in_=xgs[j][:].rearrange("p a n t -> p (a n t)"),
            )

        hbs = {}
        hsb = {}
        tps = {}
        grps = {}
        hqs = {}
        ybs = {}
        ysb = {}

        def layer1(i):
            for g in range(NG):
                hb = psum.tile([P, 512], F32, name="hb%d" % g, tag="hb%d" % g)
                nc.tensor.matmul_mx(
                    out=hb[:],
                    lhsT=xq[:, P * i : P * (i + 1)].bitcast(FP8X4),
                    lhsT_scale=xs[:, P * i : P * (i + 1)],
                    rhs=w1[:, 512 * g : 512 * (g + 1)].bitcast(FP8X4),
                    rhs_scale=planes[:, 512 * g : 512 * (g + 1)],
                    start=True,
                    stop=True,
                )
                hbs[(i, g)] = hb
            hsb[i] = ring.tile([P, NG, 2, P, 2], BF16, name="h_sb", tag="h_sb", bufs=3)

        def evac1(i, g):
            nc.vector.tensor_tensor(out=hsb[i][:, g], in0=by_t(hbs[(i, g)]), in1=b1p[:, g], op=ALU.add)

        def h_transpose(i):
            for half in range(2):
                tp = psum.tile([P, 2, 2, P], F32, name="tp%d" % half, tag="tp%d" % half)
                for gg in range(2):
                    for u in range(2):
                        words = hsb[i][:, 2 * half + gg, u].rearrange("n p e -> n (p e)").bitcast(F32)
                        nc.tensor.transpose(tp[:, gg, u, :], words, identf[:])
                tps[(i, half)] = tp
            grps[i] = ring.tile([P, NG, P, 4], BF16, name="grp", tag="grp", bufs=3, align_bytes=64)
            hqs[i] = (
                ring.tile([P, NG * P], U32, name="hq", tag="hq", bufs=3, align_bytes=64),
                ring.tile([P, NG * P], U8, name="hs", tag="hs", bufs=3, align_bytes=64),
            )

        def evac2(i, half, eng):
            src = tps[(i, half)][:].rearrange("p g u n -> p g n u")
            dst = grps[i][:, 2 * half : 2 * half + 2].bitcast(F32)
            if eng == "v":
                nc.vector.tensor_copy(out=dst, in_=src)
            else:
                nc.scalar.copy(out=dst, in_=src)

        def h_quant(i, half):
            hq, hs = hqs[i]
            nc.vector.quantize_mx(
                out=hq[:, 256 * half : 256 * (half + 1)].bitcast(FP8X4),
                scales=hs[:, 256 * half : 256 * (half + 1)],
                in_=grps[i][:, 2 * half : 2 * half + 2].rearrange("p g n t -> p (g n t)"),
            )

        def layer2(i):
            hq, hs = hqs[i]
            yb = psum.tile([P, H], F32, name="yb", tag="yb")
            for g in range(NG):
                nc.tensor.matmul_mx(
                    out=yb[:],
                    lhsT=hq[:, P * g : P * (g + 1)].bitcast(FP8X4),
                    lhsT_scale=hs[:, P * g : P * (g + 1)],
                    rhs=w2[:, g, :].bitcast(FP8X4),
                    rhs_scale=planes[:, F + H * g : F + H * (g + 1)],
                    start=(g == 0),
                    stop=(g == NG - 1),
                )
            ybs[i] = yb

        def masked_bias(i):
            nc.gpsimd.tensor_scalar(
                out=b2m[:, i, :],
                in0=b2bc[:],
                scalar1=mask[:, i : i + 1],
                scalar2=0.0,
                op0=ALU.mult,
                op1=ALU.add,
            )

        def evac3(i, on_vector):
            y = ring.tile([P, H], F32, name="y_sb", tag="y_sb", bufs=3)
            if on_vector:
                nc.vector.scalar_tensor_tensor(
                    out=y[:],
                    in0=ybs[i][:],
                    scalar=mask[:, i : i + 1],
                    in1=b2m[:, i, :],
                    op0=ALU.mult,
                    op1=ALU.add,
                )
            else:
                nc.scalar.activation(out=y[:], in_=ybs[i][:], func=ACT.Copy, scale=mask[:, i : i + 1])
                nc.gpsimd.tensor_tensor(out=y[:], in0=y[:], in1=b2m[:, i, :], op=ALU.add)
            nc.sync.dma_start(out=out_v[:, i, :], in_=y[:])

        ps0 = bias_mm(0, "yb")
        ps1 = bias_mm(512, "xb")
        nc.vector.tensor_copy(out=b1p[:, 0], in_=by_t(ps0))
        nc.scalar.copy(out=b1p[:, 1], in_=by_t(ps1))
        nc.vector.tensor_single_scalar(out=mask[:], in_=pad_sb[:], scalar=1e-9, op=ALU.is_lt)
        x_transpose(0, "hb0")
        x_transpose(1, "hb1")
        x_evac(0, "v")
        x_evac(1, "s")
        x_quant(0)
        ps2 = bias_mm(1024, "tp0")
        ps3 = bias_mm(1536, "tp1")
        ps4 = bias_mm(2048, "hb2")
        nc.scalar.copy(out=b1p[:, 2], in_=by_t(ps2))
        nc.scalar.copy(out=b1p[:, 3], in_=by_t(ps3))
        nc.scalar.activation(out=b2bc[:], in_=ps4[:], func=ACT.Copy)
        masked_bias(0)
        masked_bias(1)

        layer1(0)
        evac1(0, 0)
        evac1(0, 1)
        x_quant(1)
        evac1(0, 2)
        evac1(0, 3)
        x_transpose(2, "xb")
        x_transpose(3, "yb")
        x_evac(2, "s")
        x_evac(3, "s")

        for s in range(NT + 1):
            if s >= 1:
                h_quant(s - 1, 0)
            if s + 1 < NT:
                layer1(s + 1)
                evac1(s + 1, 0)
            if s >= 1:
                h_quant(s - 1, 1)
            if s + 1 < NT:
                evac1(s + 1, 1)
                if s == 0:
                    x_quant(2)
                    x_quant(3)
                if 1 <= s <= 4:
                    x_quant(s + 3)
                evac1(s + 1, 2)
                evac1(s + 1, 3)
            if s < NT:
                h_transpose(s)
                last = s == NT - 1
                evac2(s, 0, "s")
                evac2(s, 1, "v" if last else "s")
            if s <= 3:
                x_transpose(s + 4, "xb")
                x_evac(s + 4, "s")
            if s >= 1:
                layer2(s - 1)
                evac3(s - 1, s - 1 == NT - 1)
            if s + 2 < NT:
                masked_bias(s + 2)
